import numpy as np
import ml_dtypes


def mxq(x, axis, fmt="e4m3"):
    dtype, down = {"e4m3": (ml_dtypes.float8_e4m3fn, 7), "e5m2": (ml_dtypes.float8_e5m2, 14)}[fmt]
    v = np.moveaxis(np.asarray(x, np.float32).astype(ml_dtypes.bfloat16).astype(np.float64), axis, -1)
    blocks = v.reshape(v.shape[:-1] + (-1, 32))
    amax = np.abs(blocks).max(-1, keepdims=True)
    byte = np.maximum(np.where(amax > 0, np.frexp(amax)[1] - 1 + 127, 0) - down, 1)
    scale = np.exp2(byte - 127.0)
    codes = (blocks / scale).astype(np.float32).astype(dtype).astype(np.float64)
    return np.moveaxis((codes * scale).reshape(v.shape), -1, axis)


WIDE = False


def mx_kscale(k):
    if not WIDE:
        return np.ones(k)
    levels = np.array([10, -10, 5, -5, 0])
    a = np.random.permutation(np.resize(levels, k // 512 * 4)).reshape(k // 512, 4)
    idx = np.arange(k)
    return np.exp2(a[idx // 512, idx % 128 // 32])


BF16 = ml_dtypes.bfloat16


def bf(x):
    return np.asarray(x, np.float32).astype(BF16)


def f64(x):
    return np.asarray(x).astype(np.float64)


E2M1 = np.array([0.0, 0.5, 1.0, 1.5, 2.0, 3.0, 4.0, 6.0, -0.0, -0.5, -1.0, -1.5, -2.0, -3.0, -4.0, -6.0])


def pack_weight(w, fmt):
    k, n = w.shape
    w = f64(bf(w)).reshape(k // 32, 32, n)
    amax = np.abs(w).max(1)
    if fmt == "e4m3":
        byte = np.frexp(amax)[1] - 1 + 127 - 7
    else:
        mant, ex = np.frexp(amax / 6.0)
        byte = np.where(mant > 0.5, ex, ex - 1) + 127
    byte = np.clip(np.where(amax > 0, byte, 1), 1, 254)
    scaled = (w * np.exp2(127.0 - byte)[:, None, :]).reshape(k, n).astype(np.float32)
    by_word = np.ascontiguousarray(scaled.reshape(k // 512, 128, 4, n).transpose(0, 1, 3, 2))
    if fmt == "e4m3":
        words = by_word.astype(ml_dtypes.float8_e4m3fn).view(np.uint8)
    else:
        c = by_word.astype(ml_dtypes.float4_e2m1fn).view(np.uint8) & 0xF
        words = c[..., 0::2] | (c[..., 1::2] << 4)
    return np.ascontiguousarray(words), np.ascontiguousarray(byte.astype(np.uint8).reshape(k // 512, 16, n))


def unpack_weight(words, scales, fmt):
    g, p, n, _ = words.shape
    if fmt == "e4m3":
        vals = np.ascontiguousarray(words).view(ml_dtypes.float8_e4m3fn).astype(np.float64)
    else:
        nib = np.empty((g, p, n, 4), np.uint8)
        nib[..., 0::2] = words & 0xF
        nib[..., 1::2] = words >> 4
        vals = E2M1[nib]
    vals = vals * np.repeat(np.exp2(scales.astype(np.float64) - 127.0), 8, axis=1)[..., None]
    return vals.transpose(0, 1, 3, 2).reshape(g * 512, n)


B, S, I, Hd = 3, 512, 128, 512


def sigmoid(v):
    return 1.0 / (1.0 + np.exp(-v))


def setup_inputs():
    t = mx_kscale(Hd)
    x = bf(np.random.standard_normal((B, S, I)))
    w_emb = bf(np.random.standard_normal((Hd, I)) / np.sqrt(I) * t[:, None])
    b_emb = bf(np.random.standard_normal(Hd) * 0.5 * t)
    w_ih = np.random.standard_normal((3 * Hd, Hd)) / np.sqrt(Hd) / t[None, :]
    w_ih_words, w_ih_scales = pack_weight(np.ascontiguousarray(w_ih.T), "e4m3")
    b_ih = bf(np.random.standard_normal(3 * Hd) * 0.5)
    b_hh = bf(np.random.standard_normal(3 * Hd))
    return {"x": x,
            "w_emb": w_emb,
            "b_emb": b_emb,
            "w_ih_words": w_ih_words,
            "w_ih_scales": w_ih_scales,
            "b_ih": b_ih,
            "b_hh": b_hh}


def reference(x, w_emb, b_emb, w_ih_words, w_ih_scales, b_ih, b_hh):
    emb = f64(x) @ f64(w_emb).T + f64(b_emb)
    gi = (mxq(emb, 2, "e4m3") @ unpack_weight(w_ih_words, w_ih_scales, "e4m3")) + f64(b_ih)
    ir, iz, inn = np.split(gi, 3, axis=-1)
    b_hr, b_hz, b_hn = np.split(f64(b_hh), 3)
    r = sigmoid(ir + b_hr)
    z = sigmoid(iz + b_hz)
    n = np.tanh(inn + r * b_hn)
    h = (1.0 - z) * n
    H = h[:, :-1, :]
    h_last = h[:, -1, :][None]
    return (H, h_last)

@@ -1,0 +1,222 @@
+from contextlib import ExitStack
+
+import concourse.mybir as mybir
+from concourse.masks import make_identity
+
+FP8X4 = mybir.dt.float8_e4m3fn_x4
+BF16 = mybir.dt.bfloat16
+F32 = mybir.dt.float32
+I32 = mybir.dt.int32
+U32 = mybir.dt.uint32
+U8 = mybir.dt.uint8
+ACT = mybir.ActivationFunctionType
+ALU = mybir.AluOpType
+
+P = 128
+PACK = 4
+BATCH, SEQ, FEAT, HID = 3, 512, 128, 512
+TOK = BATCH * SEQ
+SEQ_BLOCKS = SEQ // P
+BLOCKS = BATCH * SEQ_BLOCKS
+HID_BLOCKS = HID // P
+STEPS = BATCH * HID_BLOCKS
+
+FLOPS = 2 * TOK * FEAT * HID + 2 * TOK * HID * 3 * HID
+
+
+def tile_encoderrnn_kernel(tc, x, w_emb, b_emb, w_ih_words, w_ih_scales, b_ih, b_hh, out_0, out_1):
+    nc = tc.nc
+
+    with ExitStack() as ctx:
+        ctx.enter_context(tc.manual_schedule())
+        keep = ctx.enter_context(tc.tile_pool(name="keep", bufs=1))
+        work = ctx.enter_context(tc.tile_pool(name="work", bufs=3))
+        gate_psum = ctx.enter_context(tc.psum_pool(name="gate_psum", bufs=5))
+        misc_psum = ctx.enter_context(tc.psum_pool(name="misc_psum", bufs=3))
+
+        x_rows = keep.tile([P, BLOCKS, FEAT], BF16)
+
+        def load_batch(queue, b):
+            blocks = slice(b * SEQ_BLOCKS, (b + 1) * SEQ_BLOCKS)
+            queue.dma_start(out=x_rows[:, blocks, :], in_=x[b].rearrange("(a p) i -> p a i", p=P))
+
+        load_batch(nc.sync, 0)
+        w_emb_rows = keep.tile([P, PACK, FEAT], BF16)
+        nc.scalar.dma_start(out=w_emb_rows[:], in_=w_emb.rearrange("(p t) i -> p t i", t=PACK))
+        b_emb_cols = keep.tile([P, PACK], BF16)
+        nc.scalar.dma_start(out=b_emb_cols[:], in_=b_emb.rearrange("(p t) -> p t", t=PACK))
+
+        w_scales = keep.tile([P, 3 * HID], U8, align_bytes=64)
+        nc.vector.memset(w_scales[:].bitcast(I32), 0)
+        for q in range(4):
+            nc.sync.dma_start(
+                out=w_scales[32 * q : 32 * q + 4, :].bitcast(I32),
+                in_=w_ih_scales[0, 4 * q : 4 * q + 4, :].bitcast(I32),
+            )
+        w_words = keep.tile([P, 3 * HID], U32, align_bytes=64)
+        nc.sync.dma_start(
+            out=w_words[:].bitcast(I32),
+            in_=w_ih_words[0].rearrange("p n t -> p (n t)").bitcast(I32),
+        )
+        bias_rows = keep.tile([P, P], BF16)
+        nc.vector.memset(bias_rows[:], 0.0)
+        nc.scalar.dma_start(out=bias_rows[0:12, :], in_=b_ih.rearrange("(r c) -> r c", c=P))
+        nc.scalar.dma_start(out=bias_rows[12:24, :], in_=b_hh.rearrange("(r c) -> r c", c=P))
+        for b in range(1, BATCH):
+            load_batch(nc.sync, b)
+
+        warm = keep.tile([P, 1], F32)
+        nc.vector.memset(warm[:], 0.0)
+        nc.scalar.activation(out=warm[:], in_=warm[:], func=ACT.Sigmoid)
+
+        ident_bf = keep.tile([P, P], BF16)
+        make_identity(nc, ident_bf[:])
+        ident_f32 = keep.tile([P, P], F32)
+        make_identity(nc, ident_f32[:])
+
+        w_emb_t = keep.tile([P, PACK, P], BF16)
+        x_t = keep.tile([P, TOK], BF16)
+        bias_cols = keep.tile([P, 24], F32)
+        b_in = bias_cols[:, 8:12]
+        b_hn = bias_cols[:, 20:24]
+        b_rz = keep.tile([P, 8], F32)
+        grouped = keep.tile([P, TOK, PACK], BF16, align_bytes=64)
+        emb_words = keep.tile([P, TOK], U32, align_bytes=64)
+        emb_scales = keep.tile([P, TOK], U8, align_bytes=64)
+
+        def transpose_w_emb():
+            w_emb_ps = misc_psum.tile([P, PACK, P], BF16, tag="misc")
+            for t in range(PACK):
+                nc.tensor.transpose(out=w_emb_ps[:, t, :], in_=w_emb_rows[:, t, :], identity=ident_bf[:])
+            nc.vector.tensor_copy(out=w_emb_t[:], in_=w_emb_ps[:])
+
+        def transpose_batch(b, copy):
+            x_ps = misc_psum.tile([P, SEQ], BF16, tag="misc")
+            for a in range(SEQ_BLOCKS):
+                nc.tensor.transpose(
+                    out=x_ps[:, a * P : (a + 1) * P], in_=x_rows[:, b * SEQ_BLOCKS + a, :], identity=ident_bf[:]
+                )
+            copy(out=x_t[:, b * SEQ : (b + 1) * SEQ], in_=x_ps[:])
+
+        def prepare_biases():
+            bias_ps = misc_psum.tile([P, P], BF16, tag="misc")
+            nc.tensor.transpose(out=bias_ps[:], in_=bias_rows[:], identity=ident_bf[:])
+            nc.vector.tensor_copy(out=bias_cols[:], in_=bias_ps[:, 0:24])
+            nc.vector.tensor_tensor(out=b_rz[:], in0=bias_cols[:, 0:8], in1=bias_cols[:, 12:20], op=ALU.add)
+            nc.vector.tensor_scalar(out=b_rz[:, 4:8], in0=b_rz[:, 4:8], scalar1=-1.0, scalar2=None, op0=ALU.mult)
+
+        def embed_matmuls(a):
+            steps = slice(a * P, (a + 1) * P)
+            sums = misc_psum.tile([P, PACK, P], F32, tag="misc")
+            for t in range(PACK):
+                nc.tensor.matmul(out=sums[:, t, :], lhsT=w_emb_t[:, t, :], rhs=x_t[:, steps], start=True, stop=True)
+            return sums
+
+        def embed_round(a, sums):
+            steps = slice(a * P, (a + 1) * P)
+            nc.vector.tensor_tensor(
+                out=grouped[:, steps, :],
+                in0=sums[:].rearrange("p t r -> p r t"),
+                in1=b_emb_cols[:].unsqueeze(1).to_broadcast([P, P, PACK]),
+                op=ALU.add,
+            )
+
+        def quantise_batch(b):
+            steps = slice(b * SEQ, (b + 1) * SEQ)
+            nc.vector.quantize_mx(
+                out=emb_words[:, steps].bitcast(FP8X4),
+                scales=emb_scales[:, steps],
+                in_=grouped[:, steps, :].rearrange("p r t -> p (r t)"),
+            )
+
+        def gate_matmul(step, gate):
+            b, j = divmod(step, HID_BLOCKS)
+            steps = slice(b * SEQ, (b + 1) * SEQ)
+            units = slice(gate * HID + j * P, gate * HID + (j + 1) * P)
+            acc = gate_psum.tile([P, SEQ], F32, tag="gate")
+            nc.tensor.matmul_mx(
+                out=acc[:],
+                lhsT=w_words[:, units].bitcast(FP8X4),
+                lhsT_scale=w_scales[:, units],
+                rhs=emb_words[:, steps].bitcast(FP8X4),
+                rhs_scale=emb_scales[:, steps],
+                start=True,
+                stop=True,
+            )
+            return acc
+
+        def transpose_back(h_t):
+            flipped = misc_psum.tile([P, SEQ_BLOCKS, P], F32, tag="misc")
+            for s in range(SEQ_BLOCKS):
+                nc.tensor.transpose(out=flipped[:, s, :], in_=h_t[:, s * P : (s + 1) * P], identity=ident_f32[:])
+            return flipped
+
+        def store(step, h):
+            b, j = divmod(step, HID_BLOCKS)
+            units = slice(j * P, (j + 1) * P)
+            whole = (SEQ_BLOCKS - 1) * P
+            nc.sync.dma_start(
+                out=out_0[b, 0:whole, units].rearrange("(s p) n -> p s n", p=P), in_=h[:, 0 : SEQ_BLOCKS - 1, :]
+            )
+            nc.sync.dma_start(out=out_0[b, whole : whole + 64, units], in_=h[0:64, SEQ_BLOCKS - 1, :])
+            nc.sync.dma_start(out=out_0[b, whole + 64 : SEQ - 1, units], in_=h[64 : P - 1, SEQ_BLOCKS - 1, :])
+            nc.sync.dma_start(out=out_1[0, b : b + 1, units], in_=h[P - 1 : P, SEQ_BLOCKS - 1, :])
+
+        acc_r, acc_n, acc_z, r, n, keep_new, h_t, h_ps, emb_ps = {}, {}, {}, {}, {}, {}, {}, {}, {}
+
+        def gate_matmuls(i):
+            acc_r[i] = gate_matmul(i, 0)
+            acc_n[i] = gate_matmul(i, 2)
+            acc_z[i] = gate_matmul(i, 1)
+
+        transpose_w_emb()
+        transpose_batch(0, nc.scalar.copy)
+        for a in range(SEQ_BLOCKS):
+            emb_ps[a] = embed_matmuls(a)
+            embed_round(a, emb_ps[a])
+        prepare_biases()
+        quantise_batch(0)
+        gate_matmuls(0)
+        for b in range(1, BATCH):
+            transpose_batch(b, nc.vector.tensor_copy)
+        emb_ps[SEQ_BLOCKS] = embed_matmuls(SEQ_BLOCKS)
+        embed_round(SEQ_BLOCKS, emb_ps[SEQ_BLOCKS])
+        emb_ps[SEQ_BLOCKS + 1] = embed_matmuls(SEQ_BLOCKS + 1)
+
+        AHEAD = SEQ_BLOCKS + 1
+        for i in range(STEPS + 3):
+            j = i % HID_BLOCKS
+            block = i + AHEAD
+            if i >= 3:
+                h = work.tile([P, SEQ_BLOCKS, P], F32, bufs=4)
+                nc.vector.tensor_copy(out=h[:], in_=h_ps[i - 3][:])
+                store(i - 3, h)
+            if i + 1 < STEPS:
+                gate_matmuls(i + 1)
+            if i < STEPS:
+                r[i] = work.tile([P, SEQ], F32, name="r")
+                nc.scalar.activation(out=r[i][:], in_=acc_r[i][:], func=ACT.Sigmoid, bias=b_rz[:, j : j + 1])
+            if block < BLOCKS:
+                embed_round(block, emb_ps[block])
+            if i < STEPS:
+                n[i] = work.tile([P, SEQ], F32, name="n")
+                nc.vector.scalar_tensor_tensor(
+                    out=n[i][:], in0=r[i][:], scalar=b_hn[:, j : j + 1], in1=acc_n[i][:], op0=ALU.mult, op1=ALU.add
+                )
+            if 1 <= i <= STEPS:
+                jb = (i - 1) % HID_BLOCKS
+                nc.scalar.activation(out=n[i - 1][:], in_=n[i - 1][:], func=ACT.Tanh, bias=b_in[:, jb : jb + 1])
+                h_t[i - 1] = work.tile([P, SEQ], F32, name="h_t")
+                multiplier = nc.gpsimd if block < BLOCKS else nc.vector
+                multiplier.tensor_tensor(out=h_t[i - 1][:], in0=keep_new[i - 1][:], in1=n[i - 1][:], op=ALU.mult)
+            if 2 <= i <= STEPS + 1:
+                h_ps[i - 2] = transpose_back(h_t[i - 2])
+            if i < STEPS:
+                keep_new[i] = work.tile([P, SEQ], F32, name="keep_new")
+                nc.scalar.activation(
+                    out=keep_new[i][:], in_=acc_z[i][:], func=ACT.Sigmoid, bias=b_rz[:, 4 + j : 5 + j], scale=-1.0
+                )
+            if block + 1 < BLOCKS:
+                emb_ps[block + 1] = embed_matmuls(block + 1)
+            if block < BLOCKS and block % SEQ_BLOCKS == SEQ_BLOCKS - 1:
+                quantise_batch(block // SEQ_BLOCKS)

@@ -26,25 +26,27 @@ FLOPS = 2 * TOK * FEAT * HID + 2 * TOK * HID * 3 * HID
 
 def tile_encoderrnn_kernel(tc, x, w_emb, b_emb, w_ih_words, w_ih_scales, b_ih, b_hh, out_0, out_1):
     nc = tc.nc
+    x_flat = x.flatten_outer_dims()
 
     with ExitStack() as ctx:
         ctx.enter_context(tc.manual_schedule())
         keep = ctx.enter_context(tc.tile_pool(name="keep", bufs=1))
         work = ctx.enter_context(tc.tile_pool(name="work", bufs=3))
+        out_pool = ctx.enter_context(tc.tile_pool(name="out_pool", bufs=2))
         gate_psum = ctx.enter_context(tc.psum_pool(name="gate_psum", bufs=5))
         misc_psum = ctx.enter_context(tc.psum_pool(name="misc_psum", bufs=3))
 
         x_rows = keep.tile([P, BLOCKS, FEAT], BF16)
 
-        def load_batch(queue, b):
-            blocks = slice(b * SEQ_BLOCKS, (b + 1) * SEQ_BLOCKS)
-            queue.dma_start(out=x_rows[:, blocks, :], in_=x[b].rearrange("(a p) i -> p a i", p=P))
+        def load_x_blocks(first, count):
+            nc.sync.dma_start(
+                out=x_rows[:, first : first + count, :],
+                in_=x_flat[first * P : (first + count) * P, :].rearrange("(a p) i -> p a i", p=P),
+            )
 
-        load_batch(nc.sync, 0)
+        load_x_blocks(0, SEQ_BLOCKS)
         w_emb_rows = keep.tile([P, PACK, FEAT], BF16)
         nc.scalar.dma_start(out=w_emb_rows[:], in_=w_emb.rearrange("(p t) i -> p t i", t=PACK))
-        b_emb_cols = keep.tile([P, PACK], BF16)
-        nc.scalar.dma_start(out=b_emb_cols[:], in_=b_emb.rearrange("(p t) -> p t", t=PACK))
 
         w_scales = keep.tile([P, 3 * HID], U8, align_bytes=64)
         nc.vector.memset(w_scales[:].bitcast(I32), 0)
@@ -53,26 +55,27 @@ def tile_encoderrnn_kernel(tc, x, w_emb, b_emb, w_ih_words, w_ih_scales, b_ih, b
                 out=w_scales[32 * q : 32 * q + 4, :].bitcast(I32),
                 in_=w_ih_scales[0, 4 * q : 4 * q + 4, :].bitcast(I32),
             )
+        load_x_blocks(SEQ_BLOCKS, BLOCKS - SEQ_BLOCKS)
         w_words = keep.tile([P, 3 * HID], U32, align_bytes=64)
         nc.sync.dma_start(
             out=w_words[:].bitcast(I32),
             in_=w_ih_words[0].rearrange("p n t -> p (n t)").bitcast(I32),
         )
+
+        ident_bf = keep.tile([P, P], BF16)
+        make_identity(nc, ident_bf[:])
+        b_emb_cols = keep.tile([P, PACK], BF16)
+        nc.gpsimd.dma_start(out=b_emb_cols[:], in_=b_emb.rearrange("(p t) -> p t", t=PACK))
         bias_rows = keep.tile([P, P], BF16)
         nc.vector.memset(bias_rows[:], 0.0)
-        nc.scalar.dma_start(out=bias_rows[0:12, :], in_=b_ih.rearrange("(r c) -> r c", c=P))
-        nc.scalar.dma_start(out=bias_rows[12:24, :], in_=b_hh.rearrange("(r c) -> r c", c=P))
-        for b in range(1, BATCH):
-            load_batch(nc.sync, b)
+        nc.gpsimd.dma_start(out=bias_rows[0:12, :], in_=b_ih.rearrange("(r c) -> r c", c=P))
+        nc.gpsimd.dma_start(out=bias_rows[12:24, :], in_=b_hh.rearrange("(r c) -> r c", c=P))
+        ident_f32 = keep.tile([P, P], F32)
+        make_identity(nc, ident_f32[:])
 
         warm = keep.tile([P, 1], F32)
         nc.vector.memset(warm[:], 0.0)
         nc.scalar.activation(out=warm[:], in_=warm[:], func=ACT.Sigmoid)
-
-        ident_bf = keep.tile([P, P], BF16)
-        make_identity(nc, ident_bf[:])
-        ident_f32 = keep.tile([P, P], F32)
-        make_identity(nc, ident_f32[:])
 
         w_emb_t = keep.tile([P, PACK, P], BF16)
         x_t = keep.tile([P, TOK], BF16)
@@ -83,23 +86,24 @@ def tile_encoderrnn_kernel(tc, x, w_emb, b_emb, w_ih_words, w_ih_scales, b_ih, b
         grouped = keep.tile([P, TOK, PACK], BF16, align_bytes=64)
         emb_words = keep.tile([P, TOK], U32, align_bytes=64)
         emb_scales = keep.tile([P, TOK], U8, align_bytes=64)
+        emb_ps, acc_r, acc_n, acc_z, r, n, keep_new, h_t, h_ps, h = {}, {}, {}, {}, {}, {}, {}, {}, {}, {}
 
         def transpose_w_emb():
-            w_emb_ps = misc_psum.tile([P, PACK, P], BF16, tag="misc")
+            w_emb_ps = gate_psum.tile([P, PACK, P], BF16, tag="gate")
             for t in range(PACK):
                 nc.tensor.transpose(out=w_emb_ps[:, t, :], in_=w_emb_rows[:, t, :], identity=ident_bf[:])
             nc.vector.tensor_copy(out=w_emb_t[:], in_=w_emb_ps[:])
 
-        def transpose_batch(b, copy):
-            x_ps = misc_psum.tile([P, SEQ], BF16, tag="misc")
+        def transpose_batch(b):
+            x_ps = gate_psum.tile([P, SEQ], BF16, tag="gate")
             for a in range(SEQ_BLOCKS):
                 nc.tensor.transpose(
                     out=x_ps[:, a * P : (a + 1) * P], in_=x_rows[:, b * SEQ_BLOCKS + a, :], identity=ident_bf[:]
                 )
-            copy(out=x_t[:, b * SEQ : (b + 1) * SEQ], in_=x_ps[:])
+            nc.scalar.copy(out=x_t[:, b * SEQ : (b + 1) * SEQ], in_=x_ps[:])
 
         def prepare_biases():
-            bias_ps = misc_psum.tile([P, P], BF16, tag="misc")
+            bias_ps = gate_psum.tile([P, P], BF16, tag="gate")
             nc.tensor.transpose(out=bias_ps[:], in_=bias_rows[:], identity=ident_bf[:])
             nc.vector.tensor_copy(out=bias_cols[:], in_=bias_ps[:, 0:24])
             nc.vector.tensor_tensor(out=b_rz[:], in0=bias_cols[:, 0:8], in1=bias_cols[:, 12:20], op=ALU.add)
@@ -107,30 +111,30 @@ def tile_encoderrnn_kernel(tc, x, w_emb, b_emb, w_ih_words, w_ih_scales, b_ih, b
 
         def embed_matmuls(a):
             steps = slice(a * P, (a + 1) * P)
-            sums = misc_psum.tile([P, PACK, P], F32, tag="misc")
+            emb_ps[a] = misc_psum.tile([P, PACK, P], F32, tag="misc", name="emb_ps")
             for t in range(PACK):
-                nc.tensor.matmul(out=sums[:, t, :], lhsT=w_emb_t[:, t, :], rhs=x_t[:, steps], start=True, stop=True)
-            return sums
+                nc.tensor.matmul(
+                    out=emb_ps[a][:, t, :], lhsT=w_emb_t[:, t, :], rhs=x_t[:, steps], start=True, stop=True
+                )
 
-        def embed_round(a, sums):
-            steps = slice(a * P, (a + 1) * P)
+        def embed_round(a):
             nc.vector.tensor_tensor(
-                out=grouped[:, steps, :],
-                in0=sums[:].rearrange("p t r -> p r t"),
+                out=grouped[:, a * P : (a + 1) * P, :],
+                in0=emb_ps[a][:].rearrange("p t r -> p r t"),
                 in1=b_emb_cols[:].unsqueeze(1).to_broadcast([P, P, PACK]),
                 op=ALU.add,
             )
 
-        def quantise_batch(b):
-            steps = slice(b * SEQ, (b + 1) * SEQ)
+        def quantise_block(a):
+            steps = slice(a * P, (a + 1) * P)
             nc.vector.quantize_mx(
                 out=emb_words[:, steps].bitcast(FP8X4),
                 scales=emb_scales[:, steps],
                 in_=grouped[:, steps, :].rearrange("p r t -> p (r t)"),
             )
 
-        def gate_matmul(step, gate):
-            b, j = divmod(step, HID_BLOCKS)
+        def gate_matmul(i, gate):
+            b, j = divmod(i, HID_BLOCKS)
             steps = slice(b * SEQ, (b + 1) * SEQ)
             units = slice(gate * HID + j * P, gate * HID + (j + 1) * P)
             acc = gate_psum.tile([P, SEQ], F32, tag="gate")
@@ -145,78 +149,91 @@ def tile_encoderrnn_kernel(tc, x, w_emb, b_emb, w_ih_words, w_ih_scales, b_ih, b
             )
             return acc
 
-        def transpose_back(h_t):
-            flipped = misc_psum.tile([P, SEQ_BLOCKS, P], F32, tag="misc")
-            for s in range(SEQ_BLOCKS):
-                nc.tensor.transpose(out=flipped[:, s, :], in_=h_t[:, s * P : (s + 1) * P], identity=ident_f32[:])
-            return flipped
-
-        def store(step, h):
-            b, j = divmod(step, HID_BLOCKS)
-            units = slice(j * P, (j + 1) * P)
-            whole = (SEQ_BLOCKS - 1) * P
-            nc.sync.dma_start(
-                out=out_0[b, 0:whole, units].rearrange("(s p) n -> p s n", p=P), in_=h[:, 0 : SEQ_BLOCKS - 1, :]
-            )
-            nc.sync.dma_start(out=out_0[b, whole : whole + 64, units], in_=h[0:64, SEQ_BLOCKS - 1, :])
-            nc.sync.dma_start(out=out_0[b, whole + 64 : SEQ - 1, units], in_=h[64 : P - 1, SEQ_BLOCKS - 1, :])
-            nc.sync.dma_start(out=out_1[0, b : b + 1, units], in_=h[P - 1 : P, SEQ_BLOCKS - 1, :])
-
-        acc_r, acc_n, acc_z, r, n, keep_new, h_t, h_ps, emb_ps = {}, {}, {}, {}, {}, {}, {}, {}, {}
-
         def gate_matmuls(i):
             acc_r[i] = gate_matmul(i, 0)
             acc_n[i] = gate_matmul(i, 2)
             acc_z[i] = gate_matmul(i, 1)
 
-        transpose_w_emb()
-        transpose_batch(0, nc.scalar.copy)
-        for a in range(SEQ_BLOCKS):
-            emb_ps[a] = embed_matmuls(a)
-            embed_round(a, emb_ps[a])
-        prepare_biases()
-        quantise_batch(0)
-        gate_matmuls(0)
-        for b in range(1, BATCH):
-            transpose_batch(b, nc.vector.tensor_copy)
-        emb_ps[SEQ_BLOCKS] = embed_matmuls(SEQ_BLOCKS)
-        embed_round(SEQ_BLOCKS, emb_ps[SEQ_BLOCKS])
-        emb_ps[SEQ_BLOCKS + 1] = embed_matmuls(SEQ_BLOCKS + 1)
-
-        AHEAD = SEQ_BLOCKS + 1
-        for i in range(STEPS + 3):
+        def reset_gate(i):
             j = i % HID_BLOCKS
+            r[i] = work.tile([P, SEQ], F32, name="r")
+            nc.scalar.activation(out=r[i][:], in_=acc_r[i][:], func=ACT.Sigmoid, bias=b_rz[:, j : j + 1])
+            n[i] = work.tile([P, SEQ], F32, name="n")
+            nc.vector.scalar_tensor_tensor(
+                out=n[i][:], in0=r[i][:], scalar=b_hn[:, j : j + 1], in1=acc_n[i][:], op0=ALU.mult, op1=ALU.add
+            )
+
+        def update_gate(i):
+            j = i % HID_BLOCKS
+            keep_new[i] = work.tile([P, SEQ], F32, name="keep_new")
+            nc.scalar.activation(
+                out=keep_new[i][:], in_=acc_z[i][:], func=ACT.Sigmoid, bias=b_rz[:, 4 + j : 5 + j], scale=-1.0
+            )
+
+        def new_state(i, multiplier):
+            j = i % HID_BLOCKS
+            nc.scalar.activation(out=n[i][:], in_=n[i][:], func=ACT.Tanh, bias=b_in[:, j : j + 1])
+            h_t[i] = work.tile([P, SEQ], F32, name="h_t")
+            multiplier.tensor_tensor(out=h_t[i][:], in0=keep_new[i][:], in1=n[i][:], op=ALU.mult)
+
+        def transpose_back(i):
+            h_ps[i] = misc_psum.tile([P, SEQ_BLOCKS, P], F32, tag="misc", name="h_ps")
+            for s in range(SEQ_BLOCKS):
+                nc.tensor.transpose(out=h_ps[i][:, s, :], in_=h_t[i][:, s * P : (s + 1) * P], identity=ident_f32[:])
+
+        def store(i, copy):
+            b, j = divmod(i, HID_BLOCKS)
+            units = slice(j * P, (j + 1) * P)
+            whole = SEQ_BLOCKS - 1
+            if j == 0:
+                h[b] = out_pool.tile([P, SEQ_BLOCKS, HID], F32, name="h")
+            copy(out=h[b][:, :, units], in_=h_ps[i][:])
+            nc.sync.dma_start(
+                out=out_0[b, 0 : whole * P, units].rearrange("(s p) n -> p s n", p=P), in_=h[b][:, 0:whole, units]
+            )
+            if j == HID_BLOCKS - 1:
+                nc.sync.dma_start(out=out_0[b, whole * P : whole * P + 64, :], in_=h[b][0:64, whole, :])
+                nc.sync.dma_start(out=out_1[0, b : b + 1, :], in_=h[b][P - 1 : P, whole, :])
+                nc.sync.dma_start(out=out_0[b, whole * P + 64 : SEQ - 1, :], in_=h[b][64 : P - 1, whole, :])
+
+        AHEAD = SEQ_BLOCKS + 2
+
+        transpose_w_emb()
+        transpose_batch(0)
+        for a in range(SEQ_BLOCKS):
+            embed_matmuls(a)
+            embed_round(a)
+            if a > 0:
+                quantise_block(a - 1)
+        quantise_block(SEQ_BLOCKS - 1)
+        for b in range(1, BATCH):
+            transpose_batch(b)
+        prepare_biases()
+        embed_matmuls(SEQ_BLOCKS)
+        embed_matmuls(SEQ_BLOCKS + 1)
+        gate_matmuls(0)
+        embed_round(SEQ_BLOCKS)
+        embed_round(SEQ_BLOCKS + 1)
+        quantise_block(SEQ_BLOCKS)
+        embed_matmuls(AHEAD)
+
+        for i in range(STEPS + 3):
             block = i + AHEAD
-            if i >= 3:
-                h = work.tile([P, SEQ_BLOCKS, P], F32, bufs=4)
-                nc.vector.tensor_copy(out=h[:], in_=h_ps[i - 3][:])
-                store(i - 3, h)
             if i + 1 < STEPS:
                 gate_matmuls(i + 1)
             if i < STEPS:
-                r[i] = work.tile([P, SEQ], F32, name="r")
-                nc.scalar.activation(out=r[i][:], in_=acc_r[i][:], func=ACT.Sigmoid, bias=b_rz[:, j : j + 1])
+                reset_gate(i)
             if block < BLOCKS:
-                embed_round(block, emb_ps[block])
-            if i < STEPS:
-                n[i] = work.tile([P, SEQ], F32, name="n")
-                nc.vector.scalar_tensor_tensor(
-                    out=n[i][:], in0=r[i][:], scalar=b_hn[:, j : j + 1], in1=acc_n[i][:], op0=ALU.mult, op1=ALU.add
-                )
+                embed_round(block)
+            if block - 1 < BLOCKS:
+                quantise_block(block - 1)
             if 1 <= i <= STEPS:
-                jb = (i - 1) % HID_BLOCKS
-                nc.scalar.activation(out=n[i - 1][:], in_=n[i - 1][:], func=ACT.Tanh, bias=b_in[:, jb : jb + 1])
-                h_t[i - 1] = work.tile([P, SEQ], F32, name="h_t")
-                multiplier = nc.gpsimd if block < BLOCKS else nc.vector
-                multiplier.tensor_tensor(out=h_t[i - 1][:], in0=keep_new[i - 1][:], in1=n[i - 1][:], op=ALU.mult)
+                new_state(i - 1, nc.gpsimd if block < BLOCKS else nc.vector)
             if 2 <= i <= STEPS + 1:
-                h_ps[i - 2] = transpose_back(h_t[i - 2])
+                transpose_back(i - 2)
             if i < STEPS:
-                keep_new[i] = work.tile([P, SEQ], F32, name="keep_new")
-                nc.scalar.activation(
-                    out=keep_new[i][:], in_=acc_z[i][:], func=ACT.Sigmoid, bias=b_rz[:, 4 + j : 5 + j], scale=-1.0
-                )
+                update_gate(i)
             if block + 1 < BLOCKS:
-                emb_ps[block + 1] = embed_matmuls(block + 1)
-            if block < BLOCKS and block % SEQ_BLOCKS == SEQ_BLOCKS - 1:
-                quantise_batch(block // SEQ_BLOCKS)
+                embed_matmuls(block + 1)
+            if i >= 3:
+                store(i - 3, nc.scalar.copy if i >= STEPS else nc.vector.tensor_copy)

@@ -228,7 +228,7 @@ def tile_encoderrnn_kernel(tc, x, w_emb, b_emb, w_ih_words, w_ih_scales, b_ih, b
             if block - 1 < BLOCKS:
                 quantise_block(block - 1)
             if 1 <= i <= STEPS:
-                new_state(i - 1, nc.gpsimd if block < BLOCKS else nc.vector)
+                new_state(i - 1, nc.gpsimd if i < STEPS else nc.vector)
             if 2 <= i <= STEPS + 1:
                 transpose_back(i - 2)
             if i < STEPS:
@@ -236,4 +236,4 @@ def tile_encoderrnn_kernel(tc, x, w_emb, b_emb, w_ih_words, w_ih_scales, b_ih, b
             if block + 1 < BLOCKS:
                 embed_matmuls(block + 1)
             if i >= 3:
-                store(i - 3, nc.scalar.copy if i >= STEPS else nc.vector.tensor_copy)
+                store(i - 3, nc.scalar.copy if i > STEPS else nc.vector.tensor_copy)

@@ -20,6 +20,10 @@ SEQ_BLOCKS = SEQ // P
 BLOCKS = BATCH * SEQ_BLOCKS
 HID_BLOCKS = HID // P
 STEPS = BATCH * HID_BLOCKS
+GATE_R, GATE_Z, GATE_N = 0, 1, 2
+BIAS_CHUNKS = 3
+IDLE_MATMULS = 16
+EARLY = 2
 
 FLOPS = 2 * TOK * FEAT * HID + 2 * TOK * HID * 3 * HID
 
@@ -31,8 +35,9 @@ def tile_encoderrnn_kernel(tc, x, w_emb, b_emb, w_ih_words, w_ih_scales, b_ih, b
     with ExitStack() as ctx:
         ctx.enter_context(tc.manual_schedule())
         keep = ctx.enter_context(tc.tile_pool(name="keep", bufs=1))
-        work = ctx.enter_context(tc.tile_pool(name="work", bufs=3))
-        out_pool = ctx.enter_context(tc.tile_pool(name="out_pool", bufs=2))
+        work = ctx.enter_context(tc.tile_pool(name="work", bufs=4))
+        wait_pool = ctx.enter_context(tc.tile_pool(name="wait_pool", bufs=8))
+        out_pool = ctx.enter_context(tc.tile_pool(name="out_pool", bufs=BATCH))
         gate_psum = ctx.enter_context(tc.psum_pool(name="gate_psum", bufs=5))
         misc_psum = ctx.enter_context(tc.psum_pool(name="misc_psum", bufs=3))
 
@@ -44,70 +49,91 @@ def tile_encoderrnn_kernel(tc, x, w_emb, b_emb, w_ih_words, w_ih_scales, b_ih, b
                 in_=x_flat[first * P : (first + count) * P, :].rearrange("(a p) i -> p a i", p=P),
             )
 
+        bias_rows = keep.tile([P, BIAS_CHUNKS * P], BF16)
+        nc.vector.memset(bias_rows[:], 0.0)
+        w_scales = keep.tile([P, 3 * HID], U8, align_bytes=64)
+        nc.vector.memset(w_scales[:].bitcast(I32), 0)
+        warm = keep.tile([P, 1], F32)
+        nc.vector.memset(warm[:], 0.0)
+        idle_rows = keep.tile([P, P], BF16)
+        nc.gpsimd.memset(idle_rows[:], 0.0)
+
         load_x_blocks(0, SEQ_BLOCKS)
         w_emb_rows = keep.tile([P, PACK, FEAT], BF16)
         nc.scalar.dma_start(out=w_emb_rows[:], in_=w_emb.rearrange("(p t) i -> p t i", t=PACK))
-
-        w_scales = keep.tile([P, 3 * HID], U8, align_bytes=64)
-        nc.vector.memset(w_scales[:].bitcast(I32), 0)
-        for q in range(4):
-            nc.sync.dma_start(
-                out=w_scales[32 * q : 32 * q + 4, :].bitcast(I32),
-                in_=w_ih_scales[0, 4 * q : 4 * q + 4, :].bitcast(I32),
-            )
+        b_emb_cols = keep.tile([P, PACK], BF16)
+        nc.sync.dma_start(out=b_emb_cols[:], in_=b_emb.rearrange("(p t) -> p t", t=PACK))
         load_x_blocks(SEQ_BLOCKS, BLOCKS - SEQ_BLOCKS)
+        nc.sync.dma_start(out=bias_rows[0:4, :], in_=b_ih.rearrange("(r c) -> r c", c=BIAS_CHUNKS * P))
+        nc.sync.dma_start(out=bias_rows[4:8, :], in_=b_hh.rearrange("(r c) -> r c", c=BIAS_CHUNKS * P))
         w_words = keep.tile([P, 3 * HID], U32, align_bytes=64)
         nc.sync.dma_start(
             out=w_words[:].bitcast(I32),
             in_=w_ih_words[0].rearrange("p n t -> p (n t)").bitcast(I32),
         )
+        for q in range(4):
+            nc.sync.dma_start(
+                out=w_scales[32 * q : 32 * q + 4, :].bitcast(I32),
+                in_=w_ih_scales[0, 4 * q : 4 * q + 4, :].bitcast(I32),
+            )
 
         ident_bf = keep.tile([P, P], BF16)
         make_identity(nc, ident_bf[:])
-        b_emb_cols = keep.tile([P, PACK], BF16)
-        nc.gpsimd.dma_start(out=b_emb_cols[:], in_=b_emb.rearrange("(p t) -> p t", t=PACK))
-        bias_rows = keep.tile([P, P], BF16)
-        nc.vector.memset(bias_rows[:], 0.0)
-        nc.gpsimd.dma_start(out=bias_rows[0:12, :], in_=b_ih.rearrange("(r c) -> r c", c=P))
-        nc.gpsimd.dma_start(out=bias_rows[12:24, :], in_=b_hh.rearrange("(r c) -> r c", c=P))
         ident_f32 = keep.tile([P, P], F32)
         make_identity(nc, ident_f32[:])
 
-        warm = keep.tile([P, 1], F32)
-        nc.vector.memset(warm[:], 0.0)
         nc.scalar.activation(out=warm[:], in_=warm[:], func=ACT.Sigmoid)
+
+        pick = keep.tile([P, 16], BF16)
+        nc.vector.tensor_tensor(out=pick[:, 0:4], in0=ident_bf[:, 0:4], in1=ident_bf[:, 4:8], op=ALU.add)
+        nc.vector.tensor_copy(out=pick[:, 8:16], in_=ident_bf[:, 0:8])
+        nc.vector.tensor_scalar(out=pick[:, 4:8], in0=pick[:, 0:4], scalar1=-1.0, scalar2=None, op0=ALU.mult)
 
         w_emb_t = keep.tile([P, PACK, P], BF16)
         x_t = keep.tile([P, TOK], BF16)
-        bias_cols = keep.tile([P, 24], F32)
-        b_in = bias_cols[:, 8:12]
-        b_hn = bias_cols[:, 20:24]
-        b_rz = keep.tile([P, 8], F32)
+        biases = keep.tile([P, BIAS_CHUNKS, 16], F32)
+
+        def bias(kind, block):
+            n = 4 * kind + block // BIAS_CHUNKS
+            return biases[:, block % BIAS_CHUNKS, n : n + 1]
+
         grouped = keep.tile([P, TOK, PACK], BF16, align_bytes=64)
         emb_words = keep.tile([P, TOK], U32, align_bytes=64)
         emb_scales = keep.tile([P, TOK], U8, align_bytes=64)
-        emb_ps, acc_r, acc_n, acc_z, r, n, keep_new, h_t, h_ps, h = {}, {}, {}, {}, {}, {}, {}, {}, {}, {}
+        emb_ps, acc, r, n, keep_new, h_t, h_ps, h = {}, {}, {}, {}, {}, {}, {}, {}
+
+        turned = {}
 
         def transpose_w_emb():
-            w_emb_ps = gate_psum.tile([P, PACK, P], BF16, tag="gate")
+            turned["w"] = gate_psum.tile([P, PACK, P], BF16, tag="gate", name="w_emb_ps")
             for t in range(PACK):
-                nc.tensor.transpose(out=w_emb_ps[:, t, :], in_=w_emb_rows[:, t, :], identity=ident_bf[:])
-            nc.vector.tensor_copy(out=w_emb_t[:], in_=w_emb_ps[:])
+                nc.tensor.transpose(out=turned["w"][:, t, :], in_=w_emb_rows[:, t, :], identity=ident_bf[:])
 
-        def transpose_batch(b):
-            x_ps = gate_psum.tile([P, SEQ], BF16, tag="gate")
-            for a in range(SEQ_BLOCKS):
-                nc.tensor.transpose(
-                    out=x_ps[:, a * P : (a + 1) * P], in_=x_rows[:, b * SEQ_BLOCKS + a, :], identity=ident_bf[:]
+        def copy_w_emb():
+            nc.vector.tensor_copy(out=w_emb_t[:], in_=turned["w"][:])
+
+        def transpose_blocks(first, count):
+            turned[first] = gate_psum.tile([P, count * P], BF16, tag="gate", name="x_ps")
+            for a in range(count):
+                nc.tensor.transpose(out=turned[first][:, a * P : (a + 1) * P], in_=x_rows[:, first + a, :], identity=ident_bf[:])
+
+        def copy_blocks(first, count, copy):
+            copy(out=x_t[:, first * P : (first + count) * P], in_=turned[first][:])
+
+        def bias_matmuls():
+            turned["bias"] = gate_psum.tile([P, BIAS_CHUNKS, 16], F32, tag="gate", name="bias_ps")
+            for u in range(BIAS_CHUNKS):
+                nc.tensor.matmul(
+                    out=turned["bias"][:, u, :], lhsT=bias_rows[:, u * P : (u + 1) * P], rhs=pick[:], start=True, stop=True
                 )
-            nc.scalar.copy(out=x_t[:, b * SEQ : (b + 1) * SEQ], in_=x_ps[:])
 
-        def prepare_biases():
-            bias_ps = gate_psum.tile([P, P], BF16, tag="gate")
-            nc.tensor.transpose(out=bias_ps[:], in_=bias_rows[:], identity=ident_bf[:])
-            nc.vector.tensor_copy(out=bias_cols[:], in_=bias_ps[:, 0:24])
-            nc.vector.tensor_tensor(out=b_rz[:], in0=bias_cols[:, 0:8], in1=bias_cols[:, 12:20], op=ALU.add)
-            nc.vector.tensor_scalar(out=b_rz[:, 4:8], in0=b_rz[:, 4:8], scalar1=-1.0, scalar2=None, op0=ALU.mult)
+        def copy_biases():
+            nc.vector.tensor_copy(out=biases[:], in_=turned["bias"][:])
+
+        def idle_matmuls():
+            idle_ps = misc_psum.tile([P, P], F32, tag="misc", name="idle_ps")
+            for k in range(IDLE_MATMULS):
+                nc.tensor.matmul(out=idle_ps[:], lhsT=idle_rows[:], rhs=idle_rows[:], start=True, stop=True)
 
         def embed_matmuls(a):
             steps = slice(a * P, (a + 1) * P)
@@ -125,21 +151,22 @@ def tile_encoderrnn_kernel(tc, x, w_emb, b_emb, w_ih_words, w_ih_scales, b_ih, b
                 op=ALU.add,
             )
 
-        def quantise_block(a):
-            steps = slice(a * P, (a + 1) * P)
+        def quantise_blocks(first, count):
+            steps = slice(first * P, (first + count) * P)
             nc.vector.quantize_mx(
                 out=emb_words[:, steps].bitcast(FP8X4),
                 scales=emb_scales[:, steps],
                 in_=grouped[:, steps, :].rearrange("p r t -> p (r t)"),
             )
 
-        def gate_matmul(i, gate):
+        def gate_matmul(i, gate, first=0, count=SEQ_BLOCKS):
             b, j = divmod(i, HID_BLOCKS)
-            steps = slice(b * SEQ, (b + 1) * SEQ)
             units = slice(gate * HID + j * P, gate * HID + (j + 1) * P)
-            acc = gate_psum.tile([P, SEQ], F32, tag="gate")
+            steps = slice(b * SEQ + first * P, b * SEQ + (first + count) * P)
+            if (i, gate) not in acc:
+                acc[i, gate] = gate_psum.tile([P, SEQ], F32, tag="gate", name="acc")
             nc.tensor.matmul_mx(
-                out=acc[:],
+                out=acc[i, gate][:, first * P : (first + count) * P],
                 lhsT=w_words[:, units].bitcast(FP8X4),
                 lhsT_scale=w_scales[:, units],
                 rhs=emb_words[:, steps].bitcast(FP8X4),
@@ -147,93 +174,208 @@ def tile_encoderrnn_kernel(tc, x, w_emb, b_emb, w_ih_words, w_ih_scales, b_ih, b
                 start=True,
                 stop=True,
             )
-            return acc
 
-        def gate_matmuls(i):
-            acc_r[i] = gate_matmul(i, 0)
-            acc_n[i] = gate_matmul(i, 2)
-            acc_z[i] = gate_matmul(i, 1)
-
-        def reset_gate(i):
+        def reset_gate(i, first=0, count=SEQ_BLOCKS):
             j = i % HID_BLOCKS
-            r[i] = work.tile([P, SEQ], F32, name="r")
-            nc.scalar.activation(out=r[i][:], in_=acc_r[i][:], func=ACT.Sigmoid, bias=b_rz[:, j : j + 1])
-            n[i] = work.tile([P, SEQ], F32, name="n")
-            nc.vector.scalar_tensor_tensor(
-                out=n[i][:], in0=r[i][:], scalar=b_hn[:, j : j + 1], in1=acc_n[i][:], op0=ALU.mult, op1=ALU.add
-            )
+            cols = slice(first * P, (first + count) * P)
+            if i not in r:
+                r[i] = work.tile([P, SEQ], F32, name="r")
+            nc.scalar.activation(out=r[i][:, cols], in_=acc[i, GATE_R][:, cols], func=ACT.Sigmoid, bias=bias(0, j))
 
-        def update_gate(i):
+        def update_gate(i, first=0, count=SEQ_BLOCKS):
             j = i % HID_BLOCKS
-            keep_new[i] = work.tile([P, SEQ], F32, name="keep_new")
+            cols = slice(first * P, (first + count) * P)
+            if i not in keep_new:
+                keep_new[i] = work.tile([P, SEQ], F32, name="keep_new")
             nc.scalar.activation(
-                out=keep_new[i][:], in_=acc_z[i][:], func=ACT.Sigmoid, bias=b_rz[:, 4 + j : 5 + j], scale=-1.0
+                out=keep_new[i][:, cols], in_=acc[i, GATE_Z][:, cols], func=ACT.Sigmoid, bias=bias(1, HID_BLOCKS + j), scale=-1.0
             )
 
-        def new_state(i, multiplier):
+        def candidate_sum(i, first=0, count=SEQ_BLOCKS):
             j = i % HID_BLOCKS
-            nc.scalar.activation(out=n[i][:], in_=n[i][:], func=ACT.Tanh, bias=b_in[:, j : j + 1])
-            h_t[i] = work.tile([P, SEQ], F32, name="h_t")
-            multiplier.tensor_tensor(out=h_t[i][:], in0=keep_new[i][:], in1=n[i][:], op=ALU.mult)
+            cols = slice(first * P, (first + count) * P)
+            if i not in n:
+                n[i] = work.tile([P, SEQ], F32, name="n")
+            nc.vector.scalar_tensor_tensor(
+                out=n[i][:, cols], in0=r[i][:, cols], scalar=bias(3, 2 * HID_BLOCKS + j), in1=acc[i, GATE_N][:, cols], op0=ALU.mult, op1=ALU.add
+            )
 
-        def transpose_back(i):
-            h_ps[i] = misc_psum.tile([P, SEQ_BLOCKS, P], F32, tag="misc", name="h_ps")
-            for s in range(SEQ_BLOCKS):
-                nc.tensor.transpose(out=h_ps[i][:, s, :], in_=h_t[i][:, s * P : (s + 1) * P], identity=ident_f32[:])
+        def candidate(i, first=0, count=SEQ_BLOCKS):
+            j = i % HID_BLOCKS
+            cols = slice(first * P, (first + count) * P)
+            nc.scalar.activation(out=n[i][:, cols], in_=n[i][:, cols], func=ACT.Tanh, bias=bias(2, 2 * HID_BLOCKS + j))
 
-        def store(i, copy):
+        def new_state(i, engine, first=0, count=SEQ_BLOCKS):
+            cols = slice(first * P, (first + count) * P)
+            if i not in h_t:
+                h_t[i] = wait_pool.tile([P, SEQ], F32, name="h_t")
+            engine.tensor_tensor(out=h_t[i][:, cols], in0=keep_new[i][:, cols], in1=n[i][:, cols], op=ALU.mult)
+
+        def transpose_back(i, first=0, count=SEQ_BLOCKS):
+            h_ps[i, first] = misc_psum.tile([P, count, P], F32, tag="misc", name="h_ps")
+            for s in range(count):
+                nc.tensor.transpose(
+                    out=h_ps[i, first][:, s, :], in_=h_t[i][:, (first + s) * P : (first + s + 1) * P], identity=ident_f32[:]
+                )
+
+        def copy_out(i, copy, first=0, count=SEQ_BLOCKS):
             b, j = divmod(i, HID_BLOCKS)
             units = slice(j * P, (j + 1) * P)
-            whole = SEQ_BLOCKS - 1
-            if j == 0:
+            if b not in h:
                 h[b] = out_pool.tile([P, SEQ_BLOCKS, HID], F32, name="h")
-            copy(out=h[b][:, :, units], in_=h_ps[i][:])
+            copy(out=h[b][:, first : first + count, units], in_=h_ps[i, first][:])
+
+        WHOLE = SEQ_BLOCKS - 1
+
+        def store_whole(i, first=0, count=WHOLE):
+            b, j = divmod(i, HID_BLOCKS)
+            units = slice(j * P, (j + 1) * P)
             nc.sync.dma_start(
-                out=out_0[b, 0 : whole * P, units].rearrange("(s p) n -> p s n", p=P), in_=h[b][:, 0:whole, units]
+                out=out_0[b, first * P : (first + count) * P, units].rearrange("(s p) n -> p s n", p=P),
+                in_=h[b][:, first : first + count, units],
             )
-            if j == HID_BLOCKS - 1:
-                nc.sync.dma_start(out=out_0[b, whole * P : whole * P + 64, :], in_=h[b][0:64, whole, :])
-                nc.sync.dma_start(out=out_1[0, b : b + 1, :], in_=h[b][P - 1 : P, whole, :])
-                nc.sync.dma_start(out=out_0[b, whole * P + 64 : SEQ - 1, :], in_=h[b][64 : P - 1, whole, :])
 
-        AHEAD = SEQ_BLOCKS + 2
+        def store_last_block(b):
+            nc.sync.dma_start(out=out_0[b, WHOLE * P : WHOLE * P + 64, :], in_=h[b][0:64, WHOLE, :])
+            nc.sync.dma_start(out=out_1[0, b : b + 1, :], in_=h[b][P - 1 : P, WHOLE, :])
+            nc.sync.dma_start(out=out_0[b, WHOLE * P + 64 : SEQ - 1, :], in_=h[b][64 : P - 1, WHOLE, :])
 
-        transpose_w_emb()
-        transpose_batch(0)
-        for a in range(SEQ_BLOCKS):
-            embed_matmuls(a)
-            embed_round(a)
-            if a > 0:
-                quantise_block(a - 1)
-        quantise_block(SEQ_BLOCKS - 1)
-        for b in range(1, BATCH):
-            transpose_batch(b)
-        prepare_biases()
-        embed_matmuls(SEQ_BLOCKS)
-        embed_matmuls(SEQ_BLOCKS + 1)
-        gate_matmuls(0)
-        embed_round(SEQ_BLOCKS)
-        embed_round(SEQ_BLOCKS + 1)
-        quantise_block(SEQ_BLOCKS)
-        embed_matmuls(AHEAD)
+        def span(kind, i, first, count):
+            return [(kind, i, s) for s in range(first, first + count)]
 
-        for i in range(STEPS + 3):
-            block = i + AHEAD
+        def turn_blocks(first, count):
+            return (lambda: transpose_blocks(first, count), [], [("x turned", first)])
+
+        def take_blocks(first, count, copy):
+            return (lambda: copy_blocks(first, count, copy), [("x turned", first)], [("x_t", a) for a in range(first, first + count)])
+
+        def embed(a):
+            return (lambda: embed_matmuls(a), [("x_t", a), "w_emb_t"], [("emb", a)])
+
+        def rounded(a):
+            return (lambda: embed_round(a), [("emb", a)], [("rounded", a)])
+
+        def quantised(first, count):
+            return (lambda: quantise_blocks(first, count), span("rounded", 0, 0, 0) + [("rounded", a) for a in range(first, first + count)],
+                    [("quantised", a) for a in range(first, first + count)])
+
+        def gate(i, g, first=0, count=SEQ_BLOCKS):
+            b = i // HID_BLOCKS
+            needs = [("quantised", b * SEQ_BLOCKS + s) for s in range(first, first + count)]
+            if g != GATE_N:
+                needs = needs + span(("act", g), i, 0, first)
+            return (lambda: gate_matmul(i, g, first, count), needs, span(("acc", g), i, first, count))
+
+        def gates(i):
+            return [gate(i, GATE_R), gate(i, GATE_N), gate(i, GATE_Z)]
+
+        def reset(i, first=0, count=SEQ_BLOCKS):
+            return (lambda: reset_gate(i, first, count), span(("acc", GATE_R), i, first, count) + ["biases"],
+                    span(("act", GATE_R), i, first, count))
+
+        def update(i, first=0, count=SEQ_BLOCKS):
+            return (lambda: update_gate(i, first, count), span(("acc", GATE_Z), i, first, count) + ["biases"],
+                    span(("act", GATE_Z), i, first, count))
+
+        def summed(i, first=0, count=SEQ_BLOCKS):
+            return (lambda: candidate_sum(i, first, count),
+                    span(("act", GATE_R), i, first, count) + span(("acc", GATE_N), i, first, count), span("sum", i, first, count))
+
+        def tanh(i, first=0, count=SEQ_BLOCKS):
+            return (lambda: candidate(i, first, count), span("sum", i, first, count), span("n", i, first, count))
+
+        def state(i, engine, first=0, count=SEQ_BLOCKS):
+            return (lambda: new_state(i, engine, first, count),
+                    span("n", i, first, count) + span(("act", GATE_Z), i, first, count), span("h_t", i, first, count))
+
+        def turn_back(i, first=0, count=SEQ_BLOCKS):
+            return (lambda: transpose_back(i, first, count), span("h_t", i, first, count), span("h_ps", i, first, count))
+
+        def take_out(i, copy, first=0, count=SEQ_BLOCKS):
+            return (lambda: copy_out(i, copy, first, count), span("h_ps", i, first, count), span("h", i, first, count))
+
+        def stored(i, first=0, count=WHOLE):
+            return (lambda: store_whole(i, first, count), span("h", i, first, count), [])
+
+        def stored_last(b):
+            return (lambda: store_last_block(b), [("h", b * HID_BLOCKS + j, WHOLE) for j in range(HID_BLOCKS)], [])
+
+        def weave(queues):
+            marks = set()
+            at = [0 for queue in queues]
+            moved = True
+            while moved:
+                moved = False
+                for e, queue in enumerate(queues):
+                    while at[e] < len(queue) and all(m in marks for m in queue[at[e]][1]):
+                        emit, needs, sets = queue[at[e]]
+                        emit()
+                        for m in sets:
+                            marks.add(m)
+                        at[e] += 1
+                        moved = True
+            assert all(at[e] == len(queue) for e, queue in enumerate(queues)), "the lists wait for each other"
+
+        last = STEPS - 1
+        vcopy, scopy = nc.vector.tensor_copy, nc.scalar.copy
+        HALF = SEQ_BLOCKS // 2
+
+        rounds = {2: [6], 3: [7], 4: [8, 9], 5: [10, 11]}
+        leaves = {6: [0, 1], 7: [2, 3], 8: [4, 5], 9: [6, 7], 10: [8], 11: [9]}
+
+        tensor = [(idle_matmuls, [], []), turn_blocks(0, HALF), (transpose_w_emb, [], ["w turned"]), turn_blocks(HALF, HALF),
+                  (bias_matmuls, [], ["biases summed"]), embed(0), embed(1), turn_blocks(SEQ_BLOCKS, SEQ_BLOCKS), embed(2),
+                  turn_blocks(2 * SEQ_BLOCKS, SEQ_BLOCKS), embed(3)]
+        scalar = [take_blocks(0, HALF, scopy), take_blocks(HALF, HALF, scopy), take_blocks(SEQ_BLOCKS, SEQ_BLOCKS, scopy),
+                  take_blocks(2 * SEQ_BLOCKS, SEQ_BLOCKS, scopy)]
+        vector = [(copy_w_emb, ["w turned"], ["w_emb_t"]), (copy_biases, ["biases summed"], ["biases"]),
+                  rounded(0), rounded(1), quantised(0, HALF), rounded(2), rounded(3), quantised(HALF, HALF), rounded(4), rounded(5)]
+        gpsimd = []
+        sync = []
+        for first in (0, HALF):
+            for i in range(EARLY):
+                tensor.extend([gate(i, GATE_R, first, HALF), gate(i, GATE_Z, first, HALF)])
+                scalar.extend([reset(i, first, HALF), update(i, first, HALF)])
+            if first == 0:
+                tensor.extend([embed(4), embed(5)])
+        for i in range(EARLY):
+            tensor.append(gate(i, GATE_N))
+            vector.append(summed(i))
+        vector.append(quantised(SEQ_BLOCKS, HALF))
+        tensor.extend([embed(a) for i in range(EARLY, HID_BLOCKS) for a in rounds[i]])
+        tensor.extend(gates(EARLY))
+        scalar.append(tanh(0))
+        gpsimd.append(state(0, nc.gpsimd))
+        for i in range(EARLY, STEPS):
+            if i >= HID_BLOCKS:
+                tensor.extend([embed(a) for a in rounds.get(i, [])])
             if i + 1 < STEPS:
-                gate_matmuls(i + 1)
-            if i < STEPS:
-                reset_gate(i)
-            if block < BLOCKS:
-                embed_round(block)
-            if block - 1 < BLOCKS:
-                quantise_block(block - 1)
-            if 1 <= i <= STEPS:
-                new_state(i - 1, nc.gpsimd if i < STEPS else nc.vector)
-            if 2 <= i <= STEPS + 1:
-                transpose_back(i - 2)
-            if i < STEPS:
-                update_gate(i)
-            if block + 1 < BLOCKS:
-                embed_matmuls(block + 1)
-            if i >= 3:
-                store(i - 3, nc.scalar.copy if i > STEPS else nc.vector.tensor_copy)
+                tensor.extend(gates(i + 1))
+            tensor.extend([turn_back(k) for k in leaves.get(i, [])])
+            scalar.extend([reset(i), tanh(i - 1), update(i)])
+            if i < last:
+                gpsimd.append(state(i - 1, nc.gpsimd))
+            early_round = i < HID_BLOCKS
+            if not early_round:
+                vector.append(summed(i))
+            for a in rounds.get(i, []):
+                vector.append(rounded(a))
+                if a % 2 == 1:
+                    vector.append(quantised(a - 1, 2))
+            if early_round:
+                vector.append(summed(i))
+            if i == last:
+                vector.append(state(i - 1, nc.vector))
+            for k in leaves.get(i, []):
+                vector.append(take_out(k, vcopy))
+                sync.append(stored(k))
+                if k % HID_BLOCKS == HID_BLOCKS - 1:
+                    sync.append(stored_last(k // HID_BLOCKS))
+        for first in (HALF, 0):
+            scalar.append(tanh(last, first, HALF))
+            vector.append(state(last, nc.vector, first, HALF))
+        tensor.extend([turn_back(last - 1), turn_back(last, HALF, HALF), turn_back(last, 0, HALF)])
+        scalar.extend([take_out(last - 1, scopy), take_out(last, scopy, 0, HALF)])
+        vector.append(take_out(last, vcopy, HALF, HALF))
+        sync.extend([stored(last - 1), stored(last, HALF, 1), stored_last(BATCH - 1), stored(last, 0, HALF)])
+        weave([tensor, scalar, vector, gpsimd, sync])

@@ -58,9 +58,11 @@ def tile_encoderrnn_kernel(tc, x, w_emb, b_emb, w_ih_words, w_ih_scales, b_ih, b
         idle_rows = keep.tile([P, P], BF16)
         nc.gpsimd.memset(idle_rows[:], 0.0)
 
-        load_x_blocks(0, SEQ_BLOCKS)
         w_emb_rows = keep.tile([P, PACK, FEAT], BF16)
-        nc.scalar.dma_start(out=w_emb_rows[:], in_=w_emb.rearrange("(p t) i -> p t i", t=PACK))
+        nc.sync.dma_start(out=w_emb_rows[:], in_=w_emb.rearrange("(p t) i -> p t i", t=PACK))
+        nc.scalar.dma_start(
+            out=x_rows[:, 0:SEQ_BLOCKS, :], in_=x_flat[0 : SEQ_BLOCKS * P, :].rearrange("(a p) i -> p a i", p=P)
+        )
         b_emb_cols = keep.tile([P, PACK], BF16)
         nc.sync.dma_start(out=b_emb_cols[:], in_=b_emb.rearrange("(p t) -> p t", t=PACK))
         load_x_blocks(SEQ_BLOCKS, BLOCKS - SEQ_BLOCKS)
@@ -211,8 +213,11 @@ def tile_encoderrnn_kernel(tc, x, w_emb, b_emb, w_ih_words, w_ih_scales, b_ih, b
                 h_t[i] = wait_pool.tile([P, SEQ], F32, name="h_t")
             engine.tensor_tensor(out=h_t[i][:, cols], in0=keep_new[i][:, cols], in1=n[i][:, cols], op=ALU.mult)
 
-        def transpose_back(i, first=0, count=SEQ_BLOCKS):
-            h_ps[i, first] = misc_psum.tile([P, count, P], F32, tag="misc", name="h_ps")
+        def transpose_back(i, first=0, count=SEQ_BLOCKS, spare=False):
+            if spare:
+                h_ps[i, first] = gate_psum.tile([P, count, P], F32, tag="gate", name="h_ps_spare")
+            else:
+                h_ps[i, first] = misc_psum.tile([P, count, P], F32, tag="misc", name="h_ps")
             for s in range(count):
                 nc.tensor.transpose(
                     out=h_ps[i, first][:, s, :], in_=h_t[i][:, (first + s) * P : (first + s + 1) * P], identity=ident_f32[:]
@@ -227,18 +232,20 @@ def tile_encoderrnn_kernel(tc, x, w_emb, b_emb, w_ih_words, w_ih_scales, b_ih, b
 
         WHOLE = SEQ_BLOCKS - 1
 
-        def store_whole(i, first=0, count=WHOLE):
+        def store_whole(i, queue, first=0, count=WHOLE):
             b, j = divmod(i, HID_BLOCKS)
             units = slice(j * P, (j + 1) * P)
-            nc.sync.dma_start(
+            queue.dma_start(
                 out=out_0[b, first * P : (first + count) * P, units].rearrange("(s p) n -> p s n", p=P),
                 in_=h[b][:, first : first + count, units],
             )
 
-        def store_last_block(b):
-            nc.sync.dma_start(out=out_0[b, WHOLE * P : WHOLE * P + 64, :], in_=h[b][0:64, WHOLE, :])
-            nc.sync.dma_start(out=out_1[0, b : b + 1, :], in_=h[b][P - 1 : P, WHOLE, :])
-            nc.sync.dma_start(out=out_0[b, WHOLE * P + 64 : SEQ - 1, :], in_=h[b][64 : P - 1, WHOLE, :])
+        def store_last_block(b, queue, rows):
+            if rows == 0:
+                queue.dma_start(out=out_0[b, WHOLE * P : WHOLE * P + 64, :], in_=h[b][0:64, WHOLE, :])
+                queue.dma_start(out=out_1[0, b : b + 1, :], in_=h[b][P - 1 : P, WHOLE, :])
+            else:
+                queue.dma_start(out=out_0[b, WHOLE * P + 64 : SEQ - 1, :], in_=h[b][64 : P - 1, WHOLE, :])
 
         def span(kind, i, first, count):
             return [(kind, i, s) for s in range(first, first + count)]
@@ -288,17 +295,17 @@ def tile_encoderrnn_kernel(tc, x, w_emb, b_emb, w_ih_words, w_ih_scales, b_ih, b
             return (lambda: new_state(i, engine, first, count),
                     span("n", i, first, count) + span(("act", GATE_Z), i, first, count), span("h_t", i, first, count))
 
-        def turn_back(i, first=0, count=SEQ_BLOCKS):
-            return (lambda: transpose_back(i, first, count), span("h_t", i, first, count), span("h_ps", i, first, count))
+        def turn_back(i, first=0, count=SEQ_BLOCKS, spare=False):
+            return (lambda: transpose_back(i, first, count, spare), span("h_t", i, first, count), span("h_ps", i, first, count))
 
         def take_out(i, copy, first=0, count=SEQ_BLOCKS):
             return (lambda: copy_out(i, copy, first, count), span("h_ps", i, first, count), span("h", i, first, count))
 
-        def stored(i, first=0, count=WHOLE):
-            return (lambda: store_whole(i, first, count), span("h", i, first, count), [])
+        def stored(i, queue, first=0, count=WHOLE):
+            return (lambda: store_whole(i, queue, first, count), span("h", i, first, count), [])
 
-        def stored_last(b):
-            return (lambda: store_last_block(b), [("h", b * HID_BLOCKS + j, WHOLE) for j in range(HID_BLOCKS)], [])
+        def stored_last(b, queue, rows):
+            return (lambda: store_last_block(b, queue, rows), [("h", b * HID_BLOCKS + j, WHOLE) for j in range(HID_BLOCKS)], [])
 
         def weave(queues):
             marks = set()
@@ -321,15 +328,16 @@ def tile_encoderrnn_kernel(tc, x, w_emb, b_emb, w_ih_words, w_ih_scales, b_ih, b
         HALF = SEQ_BLOCKS // 2
 
         rounds = {2: [6], 3: [7], 4: [8, 9], 5: [10, 11]}
-        leaves = {6: [0, 1], 7: [2, 3], 8: [4, 5], 9: [6, 7], 10: [8], 11: [9]}
+        leaves = {6: [0, 1], 7: [2, 3], 8: [4, 5], 9: [6, 7], 10: [8]}
 
-        tensor = [(idle_matmuls, [], []), turn_blocks(0, HALF), (transpose_w_emb, [], ["w turned"]), turn_blocks(HALF, HALF),
+        tensor = [(idle_matmuls, [], []), (transpose_w_emb, [], ["w turned"]), turn_blocks(0, HALF), turn_blocks(HALF, HALF),
                   (bias_matmuls, [], ["biases summed"]), embed(0), embed(1), turn_blocks(SEQ_BLOCKS, SEQ_BLOCKS), embed(2),
                   turn_blocks(2 * SEQ_BLOCKS, SEQ_BLOCKS), embed(3)]
         scalar = [take_blocks(0, HALF, scopy), take_blocks(HALF, HALF, scopy), take_blocks(SEQ_BLOCKS, SEQ_BLOCKS, scopy),
                   take_blocks(2 * SEQ_BLOCKS, SEQ_BLOCKS, scopy)]
         vector = [(copy_w_emb, ["w turned"], ["w_emb_t"]), (copy_biases, ["biases summed"], ["biases"]),
-                  rounded(0), rounded(1), quantised(0, HALF), rounded(2), rounded(3), quantised(HALF, HALF), rounded(4), rounded(5)]
+                  rounded(0), rounded(1), quantised(0, 1), quantised(1, 1), rounded(2), rounded(3), quantised(2, 1), quantised(3, 1),
+                  rounded(4), rounded(5)]
         gpsimd = []
         sync = []
         for first in (0, HALF):
@@ -358,24 +366,32 @@ def tile_encoderrnn_kernel(tc, x, w_emb, b_emb, w_ih_words, w_ih_scales, b_ih, b
             early_round = i < HID_BLOCKS
             if not early_round:
                 vector.append(summed(i))
-            for a in rounds.get(i, []):
-                vector.append(rounded(a))
-                if a % 2 == 1:
-                    vector.append(quantised(a - 1, 2))
+                if i - 1 >= HID_BLOCKS and i - 1 in rounds:
+                    vector.append(quantised(rounds[i - 1][0], 2))
+            vector.extend([rounded(a) for a in rounds.get(i, [])])
             if early_round:
+                if i == HID_BLOCKS - 1:
+                    vector.append(quantised(rounds[i][0] - 1, 2))
                 vector.append(summed(i))
             if i == last:
-                vector.append(state(i - 1, nc.vector))
+                tensor.append(turn_back(i - 2))
+                for first in (0, HALF):
+                    vector.append(state(i - 1, nc.vector, first, HALF))
+                    tensor.append(turn_back(i - 1, first, HALF))
             for k in leaves.get(i, []):
                 vector.append(take_out(k, vcopy))
-                sync.append(stored(k))
+                sync.append(stored(k, nc.sync))
                 if k % HID_BLOCKS == HID_BLOCKS - 1:
-                    sync.append(stored_last(k // HID_BLOCKS))
-        for first in (HALF, 0):
-            scalar.append(tanh(last, first, HALF))
-            vector.append(state(last, nc.vector, first, HALF))
-        tensor.extend([turn_back(last - 1), turn_back(last, HALF, HALF), turn_back(last, 0, HALF)])
-        scalar.extend([take_out(last - 1, scopy), take_out(last, scopy, 0, HALF)])
-        vector.append(take_out(last, vcopy, HALF, HALF))
-        sync.extend([stored(last - 1), stored(last, HALF, 1), stored_last(BATCH - 1), stored(last, 0, HALF)])
+                    sync.extend([stored_last(k // HID_BLOCKS, nc.sync, 0), stored_last(k // HID_BLOCKS, nc.sync, 1)])
+        pieces = [WHOLE] + list(range(WHOLE))
+        for a in pieces:
+            scalar.append(tanh(last, a, 1))
+            vector.append(state(last, nc.vector, a, 1))
+        for a in pieces:
+            tensor.append(turn_back(last, a, 1, True))
+            vector.append(take_out(last, vcopy, a, 1))
+        scalar.extend([take_out(last - 2, scopy), stored(last - 2, nc.scalar), take_out(last - 1, scopy, 0, HALF),
+                       take_out(last - 1, scopy, HALF, HALF), stored(last - 1, nc.scalar), stored_last(BATCH - 1, nc.scalar, 0),
+                       stored(last, nc.scalar, 0, 2), stored(last, nc.scalar, 2, 1)])
+        sync.append(stored_last(BATCH - 1, nc.sync, 1))
         weave([tensor, scalar, vector, gpsimd, sync])

@@ -353,7 +353,7 @@ def tile_encoderrnn_kernel(tc, x, w_emb, b_emb, w_ih_words, w_ih_scales, b_ih, b
         tensor.extend([embed(a) for i in range(EARLY, HID_BLOCKS) for a in rounds[i]])
         tensor.extend(gates(EARLY))
         scalar.append(tanh(0))
-        gpsimd.append(state(0, nc.gpsimd))
+        gpsimd.extend([state(0, nc.gpsimd, first, HALF) for first in (0, HALF)])
         for i in range(EARLY, STEPS):
             if i >= HID_BLOCKS:
                 tensor.extend([embed(a) for a in rounds.get(i, [])])
@@ -362,12 +362,12 @@ def tile_encoderrnn_kernel(tc, x, w_emb, b_emb, w_ih_words, w_ih_scales, b_ih, b
             tensor.extend([turn_back(k) for k in leaves.get(i, [])])
             scalar.extend([reset(i), tanh(i - 1), update(i)])
             if i < last:
-                gpsimd.append(state(i - 1, nc.gpsimd))
+                gpsimd.extend([state(i - 1, nc.gpsimd, first, HALF) for first in (0, HALF)])
             early_round = i < HID_BLOCKS
             if not early_round:
                 vector.append(summed(i))
-                if i - 1 >= HID_BLOCKS and i - 1 in rounds:
-                    vector.append(quantised(rounds[i - 1][0], 2))
+                if i - 1 in rounds and rounds[i - 1][-1] == BLOCKS - 1:
+                    vector.append(quantised(2 * SEQ_BLOCKS, SEQ_BLOCKS))
             vector.extend([rounded(a) for a in rounds.get(i, [])])
             if early_round:
                 if i == HID_BLOCKS - 1:

@@ -328,7 +328,9 @@ def tile_encoderrnn_kernel(tc, x, w_emb, b_emb, w_ih_words, w_ih_scales, b_ih, b
         HALF = SEQ_BLOCKS // 2
 
         rounds = {2: [6], 3: [7], 4: [8, 9], 5: [10, 11]}
-        leaves = {6: [0, 1], 7: [2, 3], 8: [4, 5], 9: [6, 7], 10: [8]}
+        leaves = {6: [1, 2], 7: [3, 4], 8: [5, 6], 9: [7], 10: [8], 11: [9]}
+        FIRST_OUT = HID_BLOCKS
+        OWN = 9
 
         tensor = [(idle_matmuls, [], []), (transpose_w_emb, [], ["w turned"]), turn_blocks(0, HALF), turn_blocks(HALF, HALF),
                   (bias_matmuls, [], ["biases summed"]), embed(0), embed(1), turn_blocks(SEQ_BLOCKS, SEQ_BLOCKS), embed(2),
@@ -357,13 +359,18 @@ def tile_encoderrnn_kernel(tc, x, w_emb, b_emb, w_ih_words, w_ih_scales, b_ih, b
         for i in range(EARLY, STEPS):
             if i >= HID_BLOCKS:
                 tensor.extend([embed(a) for a in rounds.get(i, [])])
+            if i + 1 == FIRST_OUT:
+                tensor.append(turn_back(0))
             if i + 1 < STEPS:
                 tensor.extend(gates(i + 1))
             tensor.extend([turn_back(k) for k in leaves.get(i, [])])
             scalar.extend([reset(i), tanh(i - 1), update(i)])
-            if i < last:
+            if i - 1 < OWN:
                 gpsimd.extend([state(i - 1, nc.gpsimd, first, HALF) for first in (0, HALF)])
             early_round = i < HID_BLOCKS
+            if i == FIRST_OUT:
+                vector.append(take_out(0, vcopy))
+                sync.append(stored(0, nc.sync))
             if not early_round:
                 vector.append(summed(i))
                 if i - 1 in rounds and rounds[i - 1][-1] == BLOCKS - 1:
@@ -373,8 +380,9 @@ def tile_encoderrnn_kernel(tc, x, w_emb, b_emb, w_ih_words, w_ih_scales, b_ih, b
                 if i == HID_BLOCKS - 1:
                     vector.append(quantised(rounds[i][0] - 1, 2))
                 vector.append(summed(i))
+            if OWN <= i - 1 < last - 1:
+                vector.append(state(i - 1, nc.vector))
             if i == last:
-                tensor.append(turn_back(i - 2))
                 for first in (0, HALF):
                     vector.append(state(i - 1, nc.vector, first, HALF))
                     tensor.append(turn_back(i - 1, first, HALF))
@@ -390,7 +398,7 @@ def tile_encoderrnn_kernel(tc, x, w_emb, b_emb, w_ih_words, w_ih_scales, b_ih, b
         for a in pieces:
             tensor.append(turn_back(last, a, 1, True))
             vector.append(take_out(last, vcopy, a, 1))
-        scalar.extend([take_out(last - 2, scopy), stored(last - 2, nc.scalar), take_out(last - 1, scopy, 0, HALF),
+        scalar.extend([take_out(last - 1, scopy, 0, HALF),
                        take_out(last - 1, scopy, HALF, HALF), stored(last - 1, nc.scalar), stored_last(BATCH - 1, nc.scalar, 0),
                        stored(last, nc.scalar, 0, 2), stored(last, nc.scalar, 2, 1)])
         sync.append(stored_last(BATCH - 1, nc.sync, 1))

@@ -346,14 +346,16 @@ def tile_encoderrnn_kernel(tc, x, w_emb, b_emb, w_ih_words, w_ih_scales, b_ih, b
             for i in range(EARLY):
                 tensor.extend([gate(i, GATE_R, first, HALF), gate(i, GATE_Z, first, HALF)])
                 scalar.extend([reset(i, first, HALF), update(i, first, HALF)])
+                if i == 0:
+                    tensor.append(gate(0, GATE_N, first, HALF))
             if first == 0:
                 tensor.extend([embed(4), embed(5)])
-        for i in range(EARLY):
-            tensor.append(gate(i, GATE_N))
-            vector.append(summed(i))
+        tensor.append(gate(1, GATE_N))
+        vector.extend([summed(i) for i in range(EARLY)])
         vector.append(quantised(SEQ_BLOCKS, HALF))
+        tensor.append(gate(EARLY, GATE_R))
         tensor.extend([embed(a) for i in range(EARLY, HID_BLOCKS) for a in rounds[i]])
-        tensor.extend(gates(EARLY))
+        tensor.extend([gate(EARLY, GATE_N), gate(EARLY, GATE_Z)])
         scalar.append(tanh(0))
         gpsimd.extend([state(0, nc.gpsimd, first, HALF) for first in (0, HALF)])
         for i in range(EARLY, STEPS):

@@ -363,9 +363,10 @@ def tile_encoderrnn_kernel(tc, x, w_emb, b_emb, w_ih_words, w_ih_scales, b_ih, b
                 tensor.extend([embed(a) for a in rounds.get(i, [])])
             if i + 1 == FIRST_OUT:
                 tensor.append(turn_back(0))
+            tensor.extend([turn_back(k) for k in leaves.get(i, [])[:-1]])
             if i + 1 < STEPS:
                 tensor.extend(gates(i + 1))
-            tensor.extend([turn_back(k) for k in leaves.get(i, [])])
+            tensor.extend([turn_back(k) for k in leaves.get(i, [])[-1:]])
             scalar.extend([reset(i), tanh(i - 1), update(i)])
             if i - 1 < OWN:
                 gpsimd.extend([state(i - 1, nc.gpsimd, first, HALF) for first in (0, HALF)])

@@ -23,6 +23,7 @@ STEPS = BATCH * HID_BLOCKS
 GATE_R, GATE_Z, GATE_N = 0, 1, 2
 BIAS_CHUNKS = 3
 IDLE_MATMULS = 16
+SCALAR_ROUNDS = (1, 3)
 EARLY = 2
 
 FLOPS = 2 * TOK * FEAT * HID + 2 * TOK * HID * 3 * HID
@@ -31,6 +32,7 @@ FLOPS = 2 * TOK * FEAT * HID + 2 * TOK * HID * 3 * HID
 def tile_encoderrnn_kernel(tc, x, w_emb, b_emb, w_ih_words, w_ih_scales, b_ih, b_hh, out_0, out_1):
     nc = tc.nc
     x_flat = x.flatten_outer_dims()
+    out_flat = out_0.flatten_outer_dims()
 
     with ExitStack() as ctx:
         ctx.enter_context(tc.manual_schedule())
@@ -41,31 +43,29 @@ def tile_encoderrnn_kernel(tc, x, w_emb, b_emb, w_ih_words, w_ih_scales, b_ih, b
         gate_psum = ctx.enter_context(tc.psum_pool(name="gate_psum", bufs=5))
         misc_psum = ctx.enter_context(tc.psum_pool(name="misc_psum", bufs=3))
 
-        x_rows = keep.tile([P, BLOCKS, FEAT], BF16)
+        x_rows = keep.tile([P, BATCH, SEQ_BLOCKS * FEAT], BF16)
 
-        def load_x_blocks(first, count):
-            nc.sync.dma_start(
+        def load_x(queue, first, count):
+            queue.dma_start(
                 out=x_rows[:, first : first + count, :],
-                in_=x_flat[first * P : (first + count) * P, :].rearrange("(a p) i -> p a i", p=P),
+                in_=x_flat[first * SEQ : (first + count) * SEQ, :].rearrange("(b p a) i -> p b (a i)", p=P, a=SEQ_BLOCKS),
             )
 
+        idle_col = keep.tile([P, 1], BF16)
+        nc.vector.memset(idle_col[:], 0.0)
         bias_rows = keep.tile([P, BIAS_CHUNKS * P], BF16)
         nc.vector.memset(bias_rows[:], 0.0)
         w_scales = keep.tile([P, 3 * HID], U8, align_bytes=64)
         nc.vector.memset(w_scales[:].bitcast(I32), 0)
         warm = keep.tile([P, 1], F32)
         nc.vector.memset(warm[:], 0.0)
-        idle_rows = keep.tile([P, P], BF16)
-        nc.gpsimd.memset(idle_rows[:], 0.0)
 
         w_emb_rows = keep.tile([P, PACK, FEAT], BF16)
         nc.sync.dma_start(out=w_emb_rows[:], in_=w_emb.rearrange("(p t) i -> p t i", t=PACK))
-        nc.scalar.dma_start(
-            out=x_rows[:, 0:SEQ_BLOCKS, :], in_=x_flat[0 : SEQ_BLOCKS * P, :].rearrange("(a p) i -> p a i", p=P)
-        )
+        load_x(nc.scalar, 0, 1)
         b_emb_cols = keep.tile([P, PACK], BF16)
         nc.sync.dma_start(out=b_emb_cols[:], in_=b_emb.rearrange("(p t) -> p t", t=PACK))
-        load_x_blocks(SEQ_BLOCKS, BLOCKS - SEQ_BLOCKS)
+        load_x(nc.sync, 1, BATCH - 1)
         nc.sync.dma_start(out=bias_rows[0:4, :], in_=b_ih.rearrange("(r c) -> r c", c=BIAS_CHUNKS * P))
         nc.sync.dma_start(out=bias_rows[4:8, :], in_=b_hh.rearrange("(r c) -> r c", c=BIAS_CHUNKS * P))
         w_words = keep.tile([P, 3 * HID], U32, align_bytes=64)
@@ -116,11 +116,14 @@ def tile_encoderrnn_kernel(tc, x, w_emb, b_emb, w_ih_words, w_ih_scales, b_ih, b
 
         def transpose_blocks(first, count):
             turned[first] = gate_psum.tile([P, count * P], BF16, tag="gate", name="x_ps")
-            for a in range(count):
-                nc.tensor.transpose(out=turned[first][:, a * P : (a + 1) * P], in_=x_rows[:, first + a, :], identity=ident_bf[:])
+            for k in range(count):
+                b, a = divmod(first + k, SEQ_BLOCKS)
+                nc.tensor.transpose(
+                    out=turned[first][:, k * P : (k + 1) * P], in_=x_rows[:, b, a * FEAT : (a + 1) * FEAT], identity=ident_bf[:]
+                )
 
-        def copy_blocks(first, count, copy):
-            copy(out=x_t[:, first * P : (first + count) * P], in_=turned[first][:])
+        def copy_blocks(first, count, copy, base):
+            copy(out=x_t[:, first * P : (first + count) * P], in_=turned[base][:, (first - base) * P : (first - base + count) * P])
 
         def bias_matmuls():
             turned["bias"] = gate_psum.tile([P, BIAS_CHUNKS, 16], F32, tag="gate", name="bias_ps")
@@ -130,22 +133,40 @@ def tile_encoderrnn_kernel(tc, x, w_emb, b_emb, w_ih_words, w_ih_scales, b_ih, b
                 )
 
         def copy_biases():
-            nc.vector.tensor_copy(out=biases[:], in_=turned["bias"][:])
+            nc.scalar.copy(out=biases[:], in_=turned["bias"][:])
 
         def idle_matmuls():
             idle_ps = misc_psum.tile([P, P], F32, tag="misc", name="idle_ps")
             for k in range(IDLE_MATMULS):
-                nc.tensor.matmul(out=idle_ps[:], lhsT=idle_rows[:], rhs=idle_rows[:], start=True, stop=True)
+                nc.tensor.matmul(out=idle_ps[:], lhsT=idle_col[:].to_broadcast([P, P]), rhs=idle_col[:].to_broadcast([P, P]), start=True, stop=True)
+
+        def embed_bias(a):
+            if a == 1:
+                emb_ps[a] = misc_psum.tile([P, PACK, P], F32, tag="misc", name="emb_ps")
+            else:
+                emb_ps[a] = gate_psum.tile([P, PACK, P], F32, tag="gate", name="emb_ps_spare")
+            nc.tensor.matmul(
+                out=emb_ps[a][:],
+                lhsT=ident_bf[:],
+                rhs=b_emb_cols[:].unsqueeze(2).to_broadcast([P, PACK, P]),
+                start=True,
+                stop=False,
+            )
 
         def embed_matmuls(a):
             steps = slice(a * P, (a + 1) * P)
-            emb_ps[a] = misc_psum.tile([P, PACK, P], F32, tag="misc", name="emb_ps")
+            biased = a in SCALAR_ROUNDS
+            if not biased:
+                emb_ps[a] = misc_psum.tile([P, PACK, P], F32, tag="misc", name="emb_ps")
             for t in range(PACK):
                 nc.tensor.matmul(
-                    out=emb_ps[a][:, t, :], lhsT=w_emb_t[:, t, :], rhs=x_t[:, steps], start=True, stop=True
+                    out=emb_ps[a][:, t, :], lhsT=w_emb_t[:, t, :], rhs=x_t[:, steps], start=not biased, stop=not biased or t == PACK - 1
                 )
 
         def embed_round(a):
+            if a in SCALAR_ROUNDS:
+                nc.scalar.copy(out=grouped[:, a * P : (a + 1) * P, :], in_=emb_ps[a][:].rearrange("p t r -> p r t"))
+                return
             nc.vector.tensor_tensor(
                 out=grouped[:, a * P : (a + 1) * P, :],
                 in0=emb_ps[a][:].rearrange("p t r -> p r t"),
@@ -235,17 +256,19 @@ def tile_encoderrnn_kernel(tc, x, w_emb, b_emb, w_ih_words, w_ih_scales, b_ih, b
         def store_whole(i, queue, first=0, count=WHOLE):
             b, j = divmod(i, HID_BLOCKS)
             units = slice(j * P, (j + 1) * P)
+            lead = min(b, 1)
+            rows = out_flat[b * (SEQ - 1) - lead : b * (SEQ - 1) - lead + SEQ, units].rearrange("(p a) n -> p a n", a=SEQ_BLOCKS)
             queue.dma_start(
-                out=out_0[b, first * P : (first + count) * P, units].rearrange("(s p) n -> p s n", p=P),
+                out=rows[:, first + lead : first + lead + count, :],
                 in_=h[b][:, first : first + count, units],
             )
 
         def store_last_block(b, queue, rows):
             if rows == 0:
-                queue.dma_start(out=out_0[b, WHOLE * P : WHOLE * P + 64, :], in_=h[b][0:64, WHOLE, :])
+                queue.dma_start(out=out_0[b, WHOLE : 64 * SEQ_BLOCKS : SEQ_BLOCKS, :], in_=h[b][0:64, WHOLE, :])
                 queue.dma_start(out=out_1[0, b : b + 1, :], in_=h[b][P - 1 : P, WHOLE, :])
             else:
-                queue.dma_start(out=out_0[b, WHOLE * P + 64 : SEQ - 1, :], in_=h[b][64 : P - 1, WHOLE, :])
+                queue.dma_start(out=out_0[b, 64 * SEQ_BLOCKS + WHOLE : SEQ - 1 : SEQ_BLOCKS, :], in_=h[b][64 : P - 1, WHOLE, :])
 
         def span(kind, i, first, count):
             return [(kind, i, s) for s in range(first, first + count)]
@@ -253,11 +276,16 @@ def tile_encoderrnn_kernel(tc, x, w_emb, b_emb, w_ih_words, w_ih_scales, b_ih, b
         def turn_blocks(first, count):
             return (lambda: transpose_blocks(first, count), [], [("x turned", first)])
 
-        def take_blocks(first, count, copy):
-            return (lambda: copy_blocks(first, count, copy), [("x turned", first)], [("x_t", a) for a in range(first, first + count)])
+        def take_blocks(first, count, copy, base=None):
+            base = first if base is None else base
+            return (lambda: copy_blocks(first, count, copy, base), [("x turned", base)], [("x_t", a) for a in range(first, first + count)])
+
+        def based(a):
+            return (lambda: embed_bias(a), [], [("based", a)])
 
         def embed(a):
-            return (lambda: embed_matmuls(a), [("x_t", a), "w_emb_t"], [("emb", a)])
+            needs = [("x_t", a), "w_emb_t"] + ([("based", a)] if a in SCALAR_ROUNDS else [])
+            return (lambda: embed_matmuls(a), needs, [("emb", a)])
 
         def rounded(a):
             return (lambda: embed_round(a), [("emb", a)], [("rounded", a)])
@@ -333,23 +361,22 @@ def tile_encoderrnn_kernel(tc, x, w_emb, b_emb, w_ih_words, w_ih_scales, b_ih, b
         OWN = 9
 
         tensor = [(idle_matmuls, [], []), (transpose_w_emb, [], ["w turned"]), turn_blocks(0, HALF), turn_blocks(HALF, HALF),
-                  (bias_matmuls, [], ["biases summed"]), embed(0), embed(1), turn_blocks(SEQ_BLOCKS, SEQ_BLOCKS), embed(2),
-                  turn_blocks(2 * SEQ_BLOCKS, SEQ_BLOCKS), embed(3)]
-        scalar = [take_blocks(0, HALF, scopy), take_blocks(HALF, HALF, scopy), take_blocks(SEQ_BLOCKS, SEQ_BLOCKS, scopy),
-                  take_blocks(2 * SEQ_BLOCKS, SEQ_BLOCKS, scopy)]
-        vector = [(copy_w_emb, ["w turned"], ["w_emb_t"]), (copy_biases, ["biases summed"], ["biases"]),
-                  rounded(0), rounded(1), quantised(0, 1), quantised(1, 1), rounded(2), rounded(3), quantised(2, 1), quantised(3, 1),
-                  rounded(4), rounded(5)]
+                  based(1), embed(0), embed(1), turn_blocks(SEQ_BLOCKS, SEQ_BLOCKS), based(3), embed(3), embed(2),
+                  (bias_matmuls, [], ["biases summed"]), turn_blocks(2 * SEQ_BLOCKS, SEQ_BLOCKS), embed(4)]
+        scalar = [take_blocks(0, 1, scopy), take_blocks(1, 1, scopy, 0), take_blocks(HALF, HALF, scopy), rounded(1), rounded(3), (copy_biases, ["biases summed"], ["biases"])]
+        vector = [(copy_w_emb, ["w turned"], ["w_emb_t"]), rounded(0), take_blocks(SEQ_BLOCKS, SEQ_BLOCKS, vcopy), quantised(0, 1), quantised(1, 1),
+                  rounded(2), take_blocks(2 * SEQ_BLOCKS, SEQ_BLOCKS, vcopy), quantised(2, 1), quantised(3, 1), rounded(4), rounded(5)]
         gpsimd = []
         sync = []
         for first in (0, HALF):
             for i in range(EARLY):
-                tensor.extend([gate(i, GATE_R, first, HALF), gate(i, GATE_Z, first, HALF)])
+                tensor.append(gate(i, GATE_R, first, HALF))
+                if first == 0 and i == EARLY - 1:
+                    tensor.append(embed(5))
+                tensor.append(gate(i, GATE_Z, first, HALF))
                 scalar.extend([reset(i, first, HALF), update(i, first, HALF)])
                 if i == 0:
                     tensor.append(gate(0, GATE_N, first, HALF))
-            if first == 0:
-                tensor.extend([embed(4), embed(5)])
         tensor.append(gate(1, GATE_N))
         vector.extend([summed(i) for i in range(EARLY)])
         vector.append(quantised(SEQ_BLOCKS, HALF))

@@ -23,7 +23,8 @@ STEPS = BATCH * HID_BLOCKS
 GATE_R, GATE_Z, GATE_N = 0, 1, 2
 BIAS_CHUNKS = 3
 IDLE_MATMULS = 16
-SCALAR_ROUNDS = (1, 3)
+HALF_ROWS = P // 2
+SCALAR_ROUNDS = ((HALF_ROWS, HALF_ROWS), (P + HALF_ROWS, HALF_ROWS), (3 * P, P))
 EARLY = 2
 
 FLOPS = 2 * TOK * FEAT * HID + 2 * TOK * HID * 3 * HID
@@ -62,7 +63,7 @@ def tile_encoderrnn_kernel(tc, x, w_emb, b_emb, w_ih_words, w_ih_scales, b_ih, b
 
         w_emb_rows = keep.tile([P, PACK, FEAT], BF16)
         nc.sync.dma_start(out=w_emb_rows[:], in_=w_emb.rearrange("(p t) i -> p t i", t=PACK))
-        load_x(nc.scalar, 0, 1)
+        load_x(nc.sync, 0, 1)
         b_emb_cols = keep.tile([P, PACK], BF16)
         nc.sync.dma_start(out=b_emb_cols[:], in_=b_emb.rearrange("(p t) -> p t", t=PACK))
         load_x(nc.sync, 1, BATCH - 1)
@@ -115,7 +116,10 @@ def tile_encoderrnn_kernel(tc, x, w_emb, b_emb, w_ih_words, w_ih_scales, b_ih, b
             nc.vector.tensor_copy(out=w_emb_t[:], in_=turned["w"][:])
 
         def transpose_blocks(first, count):
-            turned[first] = gate_psum.tile([P, count * P], BF16, tag="gate", name="x_ps")
+            if first < 2 * SEQ_BLOCKS:
+                turned[first] = gate_psum.tile([P, count * P], BF16, tag="gate", name="x_ps")
+            else:
+                turned[first] = misc_psum.tile([P, count * P], BF16, tag="misc", name="x_ps_late")
             for k in range(count):
                 b, a = divmod(first + k, SEQ_BLOCKS)
                 nc.tensor.transpose(
@@ -133,46 +137,45 @@ def tile_encoderrnn_kernel(tc, x, w_emb, b_emb, w_ih_words, w_ih_scales, b_ih, b
                 )
 
         def copy_biases():
-            nc.scalar.copy(out=biases[:], in_=turned["bias"][:])
+            nc.vector.tensor_copy(out=biases[:], in_=turned["bias"][:])
 
         def idle_matmuls():
             idle_ps = misc_psum.tile([P, P], F32, tag="misc", name="idle_ps")
             for k in range(IDLE_MATMULS):
                 nc.tensor.matmul(out=idle_ps[:], lhsT=idle_col[:].to_broadcast([P, P]), rhs=idle_col[:].to_broadcast([P, P]), start=True, stop=True)
 
-        def embed_bias(a):
-            if a == 1:
-                emb_ps[a] = misc_psum.tile([P, PACK, P], F32, tag="misc", name="emb_ps")
-            else:
-                emb_ps[a] = gate_psum.tile([P, PACK, P], F32, tag="gate", name="emb_ps_spare")
+        def embed_bias(piece):
+            first, count = piece
+            emb_ps[piece] = gate_psum.tile([P, PACK, count], F32, tag="gate", name="emb_ps_spare")
             nc.tensor.matmul(
-                out=emb_ps[a][:],
+                out=emb_ps[piece][:],
                 lhsT=ident_bf[:],
-                rhs=b_emb_cols[:].unsqueeze(2).to_broadcast([P, PACK, P]),
+                rhs=b_emb_cols[:].unsqueeze(2).to_broadcast([P, PACK, count]),
                 start=True,
                 stop=False,
             )
 
-        def embed_matmuls(a):
-            steps = slice(a * P, (a + 1) * P)
-            biased = a in SCALAR_ROUNDS
+        def embed_matmuls(piece):
+            first, count = piece
+            biased = piece in SCALAR_ROUNDS
             if not biased:
-                emb_ps[a] = misc_psum.tile([P, PACK, P], F32, tag="misc", name="emb_ps")
+                emb_ps[piece] = misc_psum.tile([P, PACK, count], F32, tag="misc", name="emb_ps")
             for t in range(PACK):
                 nc.tensor.matmul(
-                    out=emb_ps[a][:, t, :], lhsT=w_emb_t[:, t, :], rhs=x_t[:, steps], start=not biased, stop=not biased or t == PACK - 1
+                    out=emb_ps[piece][:, t, :],
+                    lhsT=w_emb_t[:, t, :],
+                    rhs=x_t[:, first : first + count],
+                    start=not biased,
+                    stop=not biased or t == PACK - 1,
                 )
 
-        def embed_round(a):
-            if a in SCALAR_ROUNDS:
-                nc.scalar.copy(out=grouped[:, a * P : (a + 1) * P, :], in_=emb_ps[a][:].rearrange("p t r -> p r t"))
+        def embed_round(piece):
+            first, count = piece
+            out, in_ = grouped[:, first : first + count, :], emb_ps[piece][:].rearrange("p t r -> p r t")
+            if piece in SCALAR_ROUNDS:
+                nc.scalar.copy(out=out, in_=in_)
                 return
-            nc.vector.tensor_tensor(
-                out=grouped[:, a * P : (a + 1) * P, :],
-                in0=emb_ps[a][:].rearrange("p t r -> p r t"),
-                in1=b_emb_cols[:].unsqueeze(1).to_broadcast([P, P, PACK]),
-                op=ALU.add,
-            )
+            nc.vector.tensor_tensor(out=out, in0=in_, in1=b_emb_cols[:].unsqueeze(1).to_broadcast([P, count, PACK]), op=ALU.add)
 
         def quantise_blocks(first, count):
             steps = slice(first * P, (first + count) * P)
@@ -280,18 +283,24 @@ def tile_encoderrnn_kernel(tc, x, w_emb, b_emb, w_ih_words, w_ih_scales, b_ih, b
             base = first if base is None else base
             return (lambda: copy_blocks(first, count, copy, base), [("x turned", base)], [("x_t", a) for a in range(first, first + count)])
 
-        def based(a):
-            return (lambda: embed_bias(a), [], [("based", a)])
+        def piece_of(a, half):
+            return (a * P, P) if half is None else (a * P + half * HALF_ROWS, HALF_ROWS)
 
-        def embed(a):
-            needs = [("x_t", a), "w_emb_t"] + ([("based", a)] if a in SCALAR_ROUNDS else [])
-            return (lambda: embed_matmuls(a), needs, [("emb", a)])
+        def based(a, half=None):
+            piece = piece_of(a, half)
+            return (lambda: embed_bias(piece), [], [("based", piece)])
 
-        def rounded(a):
-            return (lambda: embed_round(a), [("emb", a)], [("rounded", a)])
+        def embed(a, half=None):
+            piece = piece_of(a, half)
+            needs = [("x_t", a), "w_emb_t"] + ([("based", piece)] if piece in SCALAR_ROUNDS else [])
+            return (lambda: embed_matmuls(piece), needs, [("emb", piece)])
+
+        def rounded(a, half=None):
+            piece = piece_of(a, half)
+            return (lambda: embed_round(piece), [("emb", piece)], [("rounded", a, half or 0)] + ([("rounded", a, 1)] if half is None else []))
 
         def quantised(first, count):
-            return (lambda: quantise_blocks(first, count), span("rounded", 0, 0, 0) + [("rounded", a) for a in range(first, first + count)],
+            return (lambda: quantise_blocks(first, count), [("rounded", a, half) for a in range(first, first + count) for half in (0, 1)],
                     [("quantised", a) for a in range(first, first + count)])
 
         def gate(i, g, first=0, count=SEQ_BLOCKS):
@@ -361,25 +370,22 @@ def tile_encoderrnn_kernel(tc, x, w_emb, b_emb, w_ih_words, w_ih_scales, b_ih, b
         OWN = 9
 
         tensor = [(idle_matmuls, [], []), (transpose_w_emb, [], ["w turned"]), turn_blocks(0, HALF), turn_blocks(HALF, HALF),
-                  based(1), embed(0), embed(1), turn_blocks(SEQ_BLOCKS, SEQ_BLOCKS), based(3), embed(3), embed(2),
-                  (bias_matmuls, [], ["biases summed"]), turn_blocks(2 * SEQ_BLOCKS, SEQ_BLOCKS), embed(4)]
-        scalar = [take_blocks(0, 1, scopy), take_blocks(1, 1, scopy, 0), take_blocks(HALF, HALF, scopy), rounded(1), rounded(3), (copy_biases, ["biases summed"], ["biases"])]
-        vector = [(copy_w_emb, ["w turned"], ["w_emb_t"]), rounded(0), take_blocks(SEQ_BLOCKS, SEQ_BLOCKS, vcopy), quantised(0, 1), quantised(1, 1),
-                  rounded(2), take_blocks(2 * SEQ_BLOCKS, SEQ_BLOCKS, vcopy), quantised(2, 1), quantised(3, 1), rounded(4), rounded(5)]
+                  based(0, 1), based(1, 1), embed(0, 0), embed(0, 1), embed(1, 0), embed(1, 1), turn_blocks(SEQ_BLOCKS, SEQ_BLOCKS), (bias_matmuls, [], ["biases summed"]),
+                  based(3), embed(3), embed(2)]
+        scalar = [take_blocks(0, 1, scopy), take_blocks(1, 1, scopy, 0), take_blocks(HALF, HALF, scopy), rounded(0, 1), rounded(1, 1), rounded(3)]
+        vector = [(copy_w_emb, ["w turned"], ["w_emb_t"]), rounded(0, 0), rounded(1, 0), quantised(0, 1), take_blocks(SEQ_BLOCKS, SEQ_BLOCKS, vcopy), quantised(1, 1),
+                  (copy_biases, ["biases summed"], ["biases"]), rounded(2), quantised(3, 1), quantised(2, 1), rounded(4), rounded(5)]
         gpsimd = []
         sync = []
+        tensor.extend([gate(0, GATE_R, 0, HALF), gate(0, GATE_Z, 0, HALF), embed(4), gate(1, GATE_R, 0, HALF), gate(1, GATE_Z, 0, HALF),
+                       gate(0, GATE_N, 0, HALF), embed(5)])
+        tensor.extend([gate(0, GATE_R, HALF, HALF), gate(0, GATE_Z, HALF, HALF), gate(0, GATE_N, HALF, HALF), gate(1, GATE_R, HALF, HALF),
+                       gate(1, GATE_Z, HALF, HALF)])
         for first in (0, HALF):
             for i in range(EARLY):
-                tensor.append(gate(i, GATE_R, first, HALF))
-                if first == 0 and i == EARLY - 1:
-                    tensor.append(embed(5))
-                tensor.append(gate(i, GATE_Z, first, HALF))
                 scalar.extend([reset(i, first, HALF), update(i, first, HALF)])
-                if i == 0:
-                    tensor.append(gate(0, GATE_N, first, HALF))
         tensor.append(gate(1, GATE_N))
-        vector.extend([summed(i) for i in range(EARLY)])
-        vector.append(quantised(SEQ_BLOCKS, HALF))
+        vector.extend([summed(0), quantised(SEQ_BLOCKS, HALF), summed(1)])
         tensor.append(gate(EARLY, GATE_R))
         tensor.extend([embed(a) for i in range(EARLY, HID_BLOCKS) for a in rounds[i]])
         tensor.extend([gate(EARLY, GATE_N), gate(EARLY, GATE_Z)])
@@ -389,7 +395,7 @@ def tile_encoderrnn_kernel(tc, x, w_emb, b_emb, w_ih_words, w_ih_scales, b_ih, b
             if i >= HID_BLOCKS:
                 tensor.extend([embed(a) for a in rounds.get(i, [])])
             if i + 1 == FIRST_OUT:
-                tensor.append(turn_back(0))
+                tensor.extend([turn_blocks(2 * SEQ_BLOCKS, SEQ_BLOCKS), turn_back(0)])
             tensor.extend([turn_back(k) for k in leaves.get(i, [])[:-1]])
             if i + 1 < STEPS:
                 tensor.extend(gates(i + 1))
@@ -399,7 +405,7 @@ def tile_encoderrnn_kernel(tc, x, w_emb, b_emb, w_ih_words, w_ih_scales, b_ih, b
                 gpsimd.extend([state(i - 1, nc.gpsimd, first, HALF) for first in (0, HALF)])
             early_round = i < HID_BLOCKS
             if i == FIRST_OUT:
-                vector.append(take_out(0, vcopy))
+                vector.extend([take_blocks(2 * SEQ_BLOCKS, SEQ_BLOCKS, vcopy), take_out(0, vcopy)])
                 sync.append(stored(0, nc.sync))
             if not early_round:
                 vector.append(summed(i))

@@ -24,7 +24,7 @@ GATE_R, GATE_Z, GATE_N = 0, 1, 2
 BIAS_CHUNKS = 3
 IDLE_MATMULS = 16
 HALF_ROWS = P // 2
-SCALAR_ROUNDS = ((HALF_ROWS, HALF_ROWS), (P + HALF_ROWS, HALF_ROWS), (3 * P, P))
+SCALAR_ROUNDS = ((HALF_ROWS, HALF_ROWS), (P + HALF_ROWS, HALF_ROWS), (3 * P + HALF_ROWS, HALF_ROWS))
 EARLY = 2
 
 FLOPS = 2 * TOK * FEAT * HID + 2 * TOK * HID * 3 * HID
@@ -370,11 +370,11 @@ def tile_encoderrnn_kernel(tc, x, w_emb, b_emb, w_ih_words, w_ih_scales, b_ih, b
         OWN = 9
 
         tensor = [(idle_matmuls, [], []), (transpose_w_emb, [], ["w turned"]), turn_blocks(0, HALF), turn_blocks(HALF, HALF),
-                  based(0, 1), based(1, 1), embed(0, 0), embed(0, 1), embed(1, 0), embed(1, 1), turn_blocks(SEQ_BLOCKS, SEQ_BLOCKS), (bias_matmuls, [], ["biases summed"]),
-                  based(3), embed(3), embed(2)]
-        scalar = [take_blocks(0, 1, scopy), take_blocks(1, 1, scopy, 0), take_blocks(HALF, HALF, scopy), rounded(0, 1), rounded(1, 1), rounded(3)]
-        vector = [(copy_w_emb, ["w turned"], ["w_emb_t"]), rounded(0, 0), rounded(1, 0), quantised(0, 1), take_blocks(SEQ_BLOCKS, SEQ_BLOCKS, vcopy), quantised(1, 1),
-                  (copy_biases, ["biases summed"], ["biases"]), rounded(2), quantised(3, 1), quantised(2, 1), rounded(4), rounded(5)]
+                  based(0, 1), based(1, 1), embed(0, 0), embed(0, 1), embed(1, 0), embed(1, 1), turn_blocks(SEQ_BLOCKS, SEQ_BLOCKS), embed(2), (bias_matmuls, [], ["biases summed"]),
+                  based(3, 1), embed(3, 1), embed(3, 0)]
+        scalar = [take_blocks(0, 1, scopy), take_blocks(1, 1, scopy, 0), take_blocks(HALF, HALF, scopy), rounded(0, 1), rounded(1, 1), take_blocks(SEQ_BLOCKS, SEQ_BLOCKS, scopy), rounded(3, 1)]
+        vector = [(copy_w_emb, ["w turned"], ["w_emb_t"]), rounded(0, 0), rounded(1, 0), quantised(0, 1), quantised(1, 1),
+                  (copy_biases, ["biases summed"], ["biases"]), rounded(2), rounded(3, 0), quantised(2, 1), quantised(3, 1), rounded(4), rounded(5)]
         gpsimd = []
         sync = []
         tensor.extend([gate(0, GATE_R, 0, HALF), gate(0, GATE_Z, 0, HALF), embed(4), gate(1, GATE_R, 0, HALF), gate(1, GATE_Z, 0, HALF),

@@ -364,8 +364,8 @@ def tile_encoderrnn_kernel(tc, x, w_emb, b_emb, w_ih_words, w_ih_scales, b_ih, b
         vcopy, scopy = nc.vector.tensor_copy, nc.scalar.copy
         HALF = SEQ_BLOCKS // 2
 
-        rounds = {2: [6], 3: [7], 4: [8, 9], 5: [10, 11]}
-        leaves = {6: [1, 2], 7: [3, 4], 8: [5, 6], 9: [7], 10: [8], 11: [9]}
+        rounds = {2: [6], 3: [7], 4: [9, 10], 5: [11]}
+        leaves = {5: [1], 6: [2, 3], 7: [4], 8: [5, 6], 9: [7], 10: [8], 11: [9]}
         FIRST_OUT = HID_BLOCKS
         OWN = 9
 
@@ -395,17 +395,19 @@ def tile_encoderrnn_kernel(tc, x, w_emb, b_emb, w_ih_words, w_ih_scales, b_ih, b
             if i >= HID_BLOCKS:
                 tensor.extend([embed(a) for a in rounds.get(i, [])])
             if i + 1 == FIRST_OUT:
-                tensor.extend([turn_blocks(2 * SEQ_BLOCKS, SEQ_BLOCKS), turn_back(0)])
+                tensor.extend([turn_back(0), embed(8)])
             tensor.extend([turn_back(k) for k in leaves.get(i, [])[:-1]])
             if i + 1 < STEPS:
                 tensor.extend(gates(i + 1))
             tensor.extend([turn_back(k) for k in leaves.get(i, [])[-1:]])
+            if i == EARLY:
+                tensor.append(turn_blocks(2 * SEQ_BLOCKS, SEQ_BLOCKS))
             scalar.extend([reset(i), tanh(i - 1), update(i)])
             if i - 1 < OWN:
                 gpsimd.extend([state(i - 1, nc.gpsimd, first, HALF) for first in (0, HALF)])
             early_round = i < HID_BLOCKS
             if i == FIRST_OUT:
-                vector.extend([take_blocks(2 * SEQ_BLOCKS, SEQ_BLOCKS, vcopy), take_out(0, vcopy)])
+                vector.extend([take_out(0, vcopy), rounded(8)])
                 sync.append(stored(0, nc.sync))
             if not early_round:
                 vector.append(summed(i))
@@ -414,7 +416,7 @@ def tile_encoderrnn_kernel(tc, x, w_emb, b_emb, w_ih_words, w_ih_scales, b_ih, b
             vector.extend([rounded(a) for a in rounds.get(i, [])])
             if early_round:
                 if i == HID_BLOCKS - 1:
-                    vector.append(quantised(rounds[i][0] - 1, 2))
+                    vector.extend([take_blocks(2 * SEQ_BLOCKS, SEQ_BLOCKS, vcopy), quantised(rounds[i][0] - 1, 2)])
                 vector.append(summed(i))
             if OWN <= i - 1 < last - 1:
                 vector.append(state(i - 1, nc.vector))

@@ -367,6 +367,7 @@ def tile_encoderrnn_kernel(tc, x, w_emb, b_emb, w_ih_words, w_ih_scales, b_ih, b
         rounds = {2: [6], 3: [7], 4: [9, 10], 5: [11]}
         leaves = {5: [1], 6: [2, 3], 7: [4], 8: [5, 6], 9: [7], 10: [8], 11: [9]}
         FIRST_OUT = HID_BLOCKS
+        SPLIT = (1, 5)
         OWN = 9
 
         tensor = [(idle_matmuls, [], []), (transpose_w_emb, [], ["w turned"]), turn_blocks(0, HALF), turn_blocks(HALF, HALF),
@@ -390,7 +391,7 @@ def tile_encoderrnn_kernel(tc, x, w_emb, b_emb, w_ih_words, w_ih_scales, b_ih, b
         tensor.extend([embed(a) for i in range(EARLY, HID_BLOCKS) for a in rounds[i]])
         tensor.extend([gate(EARLY, GATE_N), gate(EARLY, GATE_Z)])
         scalar.append(tanh(0))
-        gpsimd.extend([state(0, nc.gpsimd, first, HALF) for first in (0, HALF)])
+        gpsimd.append(state(0, nc.gpsimd))
         for i in range(EARLY, STEPS):
             if i >= HID_BLOCKS:
                 tensor.extend([embed(a) for a in rounds.get(i, [])])
@@ -404,7 +405,10 @@ def tile_encoderrnn_kernel(tc, x, w_emb, b_emb, w_ih_words, w_ih_scales, b_ih, b
                 tensor.append(turn_blocks(2 * SEQ_BLOCKS, SEQ_BLOCKS))
             scalar.extend([reset(i), tanh(i - 1), update(i)])
             if i - 1 < OWN:
-                gpsimd.extend([state(i - 1, nc.gpsimd, first, HALF) for first in (0, HALF)])
+                if i - 1 in SPLIT:
+                    gpsimd.extend([state(i - 1, nc.gpsimd, first, HALF) for first in (0, HALF)])
+                else:
+                    gpsimd.append(state(i - 1, nc.gpsimd))
             early_round = i < HID_BLOCKS
             if i == FIRST_OUT:
                 vector.extend([take_out(0, vcopy), rounded(8)])

@@ -398,9 +398,13 @@ def tile_encoderrnn_kernel(tc, x, w_emb, b_emb, w_ih_words, w_ih_scales, b_ih, b
             if i + 1 == FIRST_OUT:
                 tensor.extend([turn_back(0), embed(8)])
             tensor.extend([turn_back(k) for k in leaves.get(i, [])[:-1]])
-            if i + 1 < STEPS:
+            if i + 1 < last:
                 tensor.extend(gates(i + 1))
-            tensor.extend([turn_back(k) for k in leaves.get(i, [])[-1:]])
+                tensor.extend([turn_back(k) for k in leaves.get(i, [])[-1:]])
+            elif i + 1 == last:
+                tensor.extend([gate(last, GATE_R)] + [turn_back(k) for k in leaves[i]] + [gate(last, GATE_N), gate(last, GATE_Z)])
+            else:
+                tensor.extend([turn_back(k) for k in leaves[i]])
             if i == EARLY:
                 tensor.append(turn_blocks(2 * SEQ_BLOCKS, SEQ_BLOCKS))
             scalar.extend([reset(i), tanh(i - 1), update(i)])

from contextlib import ExitStack

import concourse.mybir as mybir
from concourse.masks import make_identity

FP8X4 = mybir.dt.float8_e4m3fn_x4
BF16 = mybir.dt.bfloat16
F32 = mybir.dt.float32
I32 = mybir.dt.int32
U32 = mybir.dt.uint32
U8 = mybir.dt.uint8
ACT = mybir.ActivationFunctionType
ALU = mybir.AluOpType

P = 128
PACK = 4
BATCH, SEQ, FEAT, HID = 3, 512, 128, 512
TOK = BATCH * SEQ
SEQ_BLOCKS = SEQ // P
BLOCKS = BATCH * SEQ_BLOCKS
HID_BLOCKS = HID // P
STEPS = BATCH * HID_BLOCKS
GATE_R, GATE_Z, GATE_N = 0, 1, 2
BIAS_CHUNKS = 3
IDLE_MATMULS = 16
HALF_ROWS = P // 2
SCALAR_ROUNDS = ((HALF_ROWS, HALF_ROWS), (P + HALF_ROWS, HALF_ROWS), (3 * P + HALF_ROWS, HALF_ROWS))
EARLY = 2

FLOPS = 2 * TOK * FEAT * HID + 2 * TOK * HID * 3 * HID


def tile_encoderrnn_kernel(tc, x, w_emb, b_emb, w_ih_words, w_ih_scales, b_ih, b_hh, out_0, out_1):
    nc = tc.nc
    x_flat = x.flatten_outer_dims()
    out_flat = out_0.flatten_outer_dims()

    with ExitStack() as ctx:
        ctx.enter_context(tc.manual_schedule())
        keep = ctx.enter_context(tc.tile_pool(name="keep", bufs=1))
        work = ctx.enter_context(tc.tile_pool(name="work", bufs=4))
        wait_pool = ctx.enter_context(tc.tile_pool(name="wait_pool", bufs=8))
        out_pool = ctx.enter_context(tc.tile_pool(name="out_pool", bufs=BATCH))
        gate_psum = ctx.enter_context(tc.psum_pool(name="gate_psum", bufs=5))
        misc_psum = ctx.enter_context(tc.psum_pool(name="misc_psum", bufs=3))

        x_rows = keep.tile([P, BATCH, SEQ_BLOCKS * FEAT], BF16)

        def load_x(queue, first, count):
            queue.dma_start(
                out=x_rows[:, first : first + count, :],
                in_=x_flat[first * SEQ : (first + count) * SEQ, :].rearrange("(b p a) i -> p b (a i)", p=P, a=SEQ_BLOCKS),
            )

        idle_col = keep.tile([P, 1], BF16)
        nc.vector.memset(idle_col[:], 0.0)
        bias_rows = keep.tile([P, BIAS_CHUNKS * P], BF16)
        nc.vector.memset(bias_rows[:], 0.0)
        w_scales = keep.tile([P, 3 * HID], U8, align_bytes=64)
        nc.vector.memset(w_scales[:].bitcast(I32), 0)
        warm = keep.tile([P, 1], F32)
        nc.vector.memset(warm[:], 0.0)

        w_emb_rows = keep.tile([P, PACK, FEAT], BF16)
        nc.sync.dma_start(out=w_emb_rows[:], in_=w_emb.rearrange("(p t) i -> p t i", t=PACK))
        load_x(nc.sync, 0, 1)
        b_emb_cols = keep.tile([P, PACK], BF16)
        nc.sync.dma_start(out=b_emb_cols[:], in_=b_emb.rearrange("(p t) -> p t", t=PACK))
        load_x(nc.sync, 1, BATCH - 1)
        nc.sync.dma_start(out=bias_rows[0:4, :], in_=b_ih.rearrange("(r c) -> r c", c=BIAS_CHUNKS * P))
        nc.sync.dma_start(out=bias_rows[4:8, :], in_=b_hh.rearrange("(r c) -> r c", c=BIAS_CHUNKS * P))
        w_words = keep.tile([P, 3 * HID], U32, align_bytes=64)
        nc.sync.dma_start(
            out=w_words[:].bitcast(I32),
            in_=w_ih_words[0].rearrange("p n t -> p (n t)").bitcast(I32),
        )
        for q in range(4):
            nc.sync.dma_start(
                out=w_scales[32 * q : 32 * q + 4, :].bitcast(I32),
                in_=w_ih_scales[0, 4 * q : 4 * q + 4, :].bitcast(I32),
            )

        ident_bf = keep.tile([P, P], BF16)
        make_identity(nc, ident_bf[:])
        ident_f32 = keep.tile([P, P], F32)
        make_identity(nc, ident_f32[:])

        nc.scalar.activation(out=warm[:], in_=warm[:], func=ACT.Sigmoid)

        pick = keep.tile([P, 16], BF16)
        nc.vector.tensor_tensor(out=pick[:, 0:4], in0=ident_bf[:, 0:4], in1=ident_bf[:, 4:8], op=ALU.add)
        nc.vector.tensor_copy(out=pick[:, 8:16], in_=ident_bf[:, 0:8])
        nc.vector.tensor_scalar(out=pick[:, 4:8], in0=pick[:, 0:4], scalar1=-1.0, scalar2=None, op0=ALU.mult)

        w_emb_t = keep.tile([P, PACK, P], BF16)
        x_t = keep.tile([P, TOK], BF16)
        biases = keep.tile([P, BIAS_CHUNKS, 16], F32)

        def bias(kind, block):
            n = 4 * kind + block // BIAS_CHUNKS
            return biases[:, block % BIAS_CHUNKS, n : n + 1]

        grouped = keep.tile([P, TOK, PACK], BF16, align_bytes=64)
        emb_words = keep.tile([P, TOK], U32, align_bytes=64)
        emb_scales = keep.tile([P, TOK], U8, align_bytes=64)
        emb_ps, acc, r, n, keep_new, h_t, h_ps, h = {}, {}, {}, {}, {}, {}, {}, {}

        turned = {}

        def transpose_w_emb():
            turned["w"] = gate_psum.tile([P, PACK, P], BF16, tag="gate", name="w_emb_ps")
            for t in range(PACK):
                nc.tensor.transpose(out=turned["w"][:, t, :], in_=w_emb_rows[:, t, :], identity=ident_bf[:])

        def copy_w_emb():
            nc.vector.tensor_copy(out=w_emb_t[:], in_=turned["w"][:])

        def transpose_blocks(first, count):
            if first < 2 * SEQ_BLOCKS:
                turned[first] = gate_psum.tile([P, count * P], BF16, tag="gate", name="x_ps")
            else:
                turned[first] = misc_psum.tile([P, count * P], BF16, tag="misc", name="x_ps_late")
            for k in range(count):
                b, a = divmod(first + k, SEQ_BLOCKS)
                nc.tensor.transpose(
                    out=turned[first][:, k * P : (k + 1) * P], in_=x_rows[:, b, a * FEAT : (a + 1) * FEAT], identity=ident_bf[:]
                )

        def copy_blocks(first, count, copy, base):
            copy(out=x_t[:, first * P : (first + count) * P], in_=turned[base][:, (first - base) * P : (first - base + count) * P])

        def bias_matmuls():
            turned["bias"] = gate_psum.tile([P, BIAS_CHUNKS, 16], F32, tag="gate", name="bias_ps")
            for u in range(BIAS_CHUNKS):
                nc.tensor.matmul(
                    out=turned["bias"][:, u, :], lhsT=bias_rows[:, u * P : (u + 1) * P], rhs=pick[:], start=True, stop=True
                )

        def copy_biases():
            nc.vector.tensor_copy(out=biases[:], in_=turned["bias"][:])

        def idle_matmuls():
            idle_ps = misc_psum.tile([P, P], F32, tag="misc", name="idle_ps")
            for k in range(IDLE_MATMULS):
                nc.tensor.matmul(out=idle_ps[:], lhsT=idle_col[:].to_broadcast([P, P]), rhs=idle_col[:].to_broadcast([P, P]), start=True, stop=True)

        def embed_bias(piece):
            first, count = piece
            emb_ps[piece] = gate_psum.tile([P, PACK, count], F32, tag="gate", name="emb_ps_spare")
            nc.tensor.matmul(
                out=emb_ps[piece][:],
                lhsT=ident_bf[:],
                rhs=b_emb_cols[:].unsqueeze(2).to_broadcast([P, PACK, count]),
                start=True,
                stop=False,
            )

        def embed_matmuls(piece):
            first, count = piece
            biased = piece in SCALAR_ROUNDS
            if not biased:
                emb_ps[piece] = misc_psum.tile([P, PACK, count], F32, tag="misc", name="emb_ps")
            for t in range(PACK):
                nc.tensor.matmul(
                    out=emb_ps[piece][:, t, :],
                    lhsT=w_emb_t[:, t, :],
                    rhs=x_t[:, first : first + count],
                    start=not biased,
                    stop=not biased or t == PACK - 1,
                )

        def embed_round(piece):
            first, count = piece
            out, in_ = grouped[:, first : first + count, :], emb_ps[piece][:].rearrange("p t r -> p r t")
            if piece in SCALAR_ROUNDS:
                nc.scalar.copy(out=out, in_=in_)
                return
            nc.vector.tensor_tensor(out=out, in0=in_, in1=b_emb_cols[:].unsqueeze(1).to_broadcast([P, count, PACK]), op=ALU.add)

        def quantise_blocks(first, count):
            steps = slice(first * P, (first + count) * P)
            nc.vector.quantize_mx(
                out=emb_words[:, steps].bitcast(FP8X4),
                scales=emb_scales[:, steps],
                in_=grouped[:, steps, :].rearrange("p r t -> p (r t)"),
            )

        def gate_matmul(i, gate, first=0, count=SEQ_BLOCKS):
            b, j = divmod(i, HID_BLOCKS)
            units = slice(gate * HID + j * P, gate * HID + (j + 1) * P)
            steps = slice(b * SEQ + first * P, b * SEQ + (first + count) * P)
            if (i, gate) not in acc:
                acc[i, gate] = gate_psum.tile([P, SEQ], F32, tag="gate", name="acc")
            nc.tensor.matmul_mx(
                out=acc[i, gate][:, first * P : (first + count) * P],
                lhsT=w_words[:, units].bitcast(FP8X4),
                lhsT_scale=w_scales[:, units],
                rhs=emb_words[:, steps].bitcast(FP8X4),
                rhs_scale=emb_scales[:, steps],
                start=True,
                stop=True,
            )

        def reset_gate(i, first=0, count=SEQ_BLOCKS):
            j = i % HID_BLOCKS
            cols = slice(first * P, (first + count) * P)
            if i not in r:
                r[i] = work.tile([P, SEQ], F32, name="r")
            nc.scalar.activation(out=r[i][:, cols], in_=acc[i, GATE_R][:, cols], func=ACT.Sigmoid, bias=bias(0, j))

        def update_gate(i, first=0, count=SEQ_BLOCKS):
            j = i % HID_BLOCKS
            cols = slice(first * P, (first + count) * P)
            if i not in keep_new:
                keep_new[i] = work.tile([P, SEQ], F32, name="keep_new")
            nc.scalar.activation(
                out=keep_new[i][:, cols], in_=acc[i, GATE_Z][:, cols], func=ACT.Sigmoid, bias=bias(1, HID_BLOCKS + j), scale=-1.0
            )

        def candidate_sum(i, first=0, count=SEQ_BLOCKS):
            j = i % HID_BLOCKS
            cols = slice(first * P, (first + count) * P)
            if i not in n:
                n[i] = work.tile([P, SEQ], F32, name="n")
            nc.vector.scalar_tensor_tensor(
                out=n[i][:, cols], in0=r[i][:, cols], scalar=bias(3, 2 * HID_BLOCKS + j), in1=acc[i, GATE_N][:, cols], op0=ALU.mult, op1=ALU.add
            )

        def candidate(i, first=0, count=SEQ_BLOCKS):
            j = i % HID_BLOCKS
            cols = slice(first * P, (first + count) * P)
            nc.scalar.activation(out=n[i][:, cols], in_=n[i][:, cols], func=ACT.Tanh, bias=bias(2, 2 * HID_BLOCKS + j))

        def new_state(i, engine, first=0, count=SEQ_BLOCKS):
            cols = slice(first * P, (first + count) * P)
            if i not in h_t:
                h_t[i] = wait_pool.tile([P, SEQ], F32, name="h_t")
            engine.tensor_tensor(out=h_t[i][:, cols], in0=keep_new[i][:, cols], in1=n[i][:, cols], op=ALU.mult)

        def transpose_back(i, first=0, count=SEQ_BLOCKS, spare=False):
            if spare:
                h_ps[i, first] = gate_psum.tile([P, count, P], F32, tag="gate", name="h_ps_spare")
            else:
                h_ps[i, first] = misc_psum.tile([P, count, P], F32, tag="misc", name="h_ps")
            for s in range(count):
                nc.tensor.transpose(
                    out=h_ps[i, first][:, s, :], in_=h_t[i][:, (first + s) * P : (first + s + 1) * P], identity=ident_f32[:]
                )

        def copy_out(i, copy, first=0, count=SEQ_BLOCKS):
            b, j = divmod(i, HID_BLOCKS)
            units = slice(j * P, (j + 1) * P)
            if b not in h:
                h[b] = out_pool.tile([P, SEQ_BLOCKS, HID], F32, name="h")
            copy(out=h[b][:, first : first + count, units], in_=h_ps[i, first][:])

        WHOLE = SEQ_BLOCKS - 1

        def store_whole(i, queue, first=0, count=WHOLE):
            b, j = divmod(i, HID_BLOCKS)
            units = slice(j * P, (j + 1) * P)
            lead = min(b, 1)
            rows = out_flat[b * (SEQ - 1) - lead : b * (SEQ - 1) - lead + SEQ, units].rearrange("(p a) n -> p a n", a=SEQ_BLOCKS)
            queue.dma_start(
                out=rows[:, first + lead : first + lead + count, :],
                in_=h[b][:, first : first + count, units],
            )

        def store_last_block(b, queue, rows):
            if rows == 0:
                queue.dma_start(out=out_0[b, WHOLE : 64 * SEQ_BLOCKS : SEQ_BLOCKS, :], in_=h[b][0:64, WHOLE, :])
                queue.dma_start(out=out_1[0, b : b + 1, :], in_=h[b][P - 1 : P, WHOLE, :])
            else:
                queue.dma_start(out=out_0[b, 64 * SEQ_BLOCKS + WHOLE : SEQ - 1 : SEQ_BLOCKS, :], in_=h[b][64 : P - 1, WHOLE, :])

        def span(kind, i, first, count):
            return [(kind, i, s) for s in range(first, first + count)]

        def turn_blocks(first, count):
            return (lambda: transpose_blocks(first, count), [], [("x turned", first)])

        def take_blocks(first, count, copy, base=None):
            base = first if base is None else base
            return (lambda: copy_blocks(first, count, copy, base), [("x turned", base)], [("x_t", a) for a in range(first, first + count)])

        def piece_of(a, half):
            return (a * P, P) if half is None else (a * P + half * HALF_ROWS, HALF_ROWS)

        def based(a, half=None):
            piece = piece_of(a, half)
            return (lambda: embed_bias(piece), [], [("based", piece)])

        def embed(a, half=None):
            piece = piece_of(a, half)
            needs = [("x_t", a), "w_emb_t"] + ([("based", piece)] if piece in SCALAR_ROUNDS else [])
            return (lambda: embed_matmuls(piece), needs, [("emb", piece)])

        def rounded(a, half=None):
            piece = piece_of(a, half)
            return (lambda: embed_round(piece), [("emb", piece)], [("rounded", a, half or 0)] + ([("rounded", a, 1)] if half is None else []))

        def quantised(first, count):
            return (lambda: quantise_blocks(first, count), [("rounded", a, half) for a in range(first, first + count) for half in (0, 1)],
                    [("quantised", a) for a in range(first, first + count)])

        def gate(i, g, first=0, count=SEQ_BLOCKS):
            b = i // HID_BLOCKS
            needs = [("quantised", b * SEQ_BLOCKS + s) for s in range(first, first + count)]
            if g != GATE_N:
                needs = needs + span(("act", g), i, 0, first)
            return (lambda: gate_matmul(i, g, first, count), needs, span(("acc", g), i, first, count))

        def gates(i):
            return [gate(i, GATE_R), gate(i, GATE_N), gate(i, GATE_Z)]

        def reset(i, first=0, count=SEQ_BLOCKS):
            return (lambda: reset_gate(i, first, count), span(("acc", GATE_R), i, first, count) + ["biases"],
                    span(("act", GATE_R), i, first, count))

        def update(i, first=0, count=SEQ_BLOCKS):
            return (lambda: update_gate(i, first, count), span(("acc", GATE_Z), i, first, count) + ["biases"],
                    span(("act", GATE_Z), i, first, count))

        def summed(i, first=0, count=SEQ_BLOCKS):
            return (lambda: candidate_sum(i, first, count),
                    span(("act", GATE_R), i, first, count) + span(("acc", GATE_N), i, first, count), span("sum", i, first, count))

        def tanh(i, first=0, count=SEQ_BLOCKS):
            return (lambda: candidate(i, first, count), span("sum", i, first, count), span("n", i, first, count))

        def state(i, engine, first=0, count=SEQ_BLOCKS):
            return (lambda: new_state(i, engine, first, count),
                    span("n", i, first, count) + span(("act", GATE_Z), i, first, count), span("h_t", i, first, count))

        def turn_back(i, first=0, count=SEQ_BLOCKS, spare=False):
            return (lambda: transpose_back(i, first, count, spare), span("h_t", i, first, count), span("h_ps", i, first, count))

        def take_out(i, copy, first=0, count=SEQ_BLOCKS):
            return (lambda: copy_out(i, copy, first, count), span("h_ps", i, first, count), span("h", i, first, count))

        def stored(i, queue, first=0, count=WHOLE):
            return (lambda: store_whole(i, queue, first, count), span("h", i, first, count), [])

        def stored_last(b, queue, rows):
            return (lambda: store_last_block(b, queue, rows), [("h", b * HID_BLOCKS + j, WHOLE) for j in range(HID_BLOCKS)], [])

        def weave(queues):
            marks = set()
            at = [0 for queue in queues]
            moved = True
            while moved:
                moved = False
                for e, queue in enumerate(queues):
                    while at[e] < len(queue) and all(m in marks for m in queue[at[e]][1]):
                        emit, needs, sets = queue[at[e]]
                        emit()
                        for m in sets:
                            marks.add(m)
                        at[e] += 1
                        moved = True
            assert all(at[e] == len(queue) for e, queue in enumerate(queues)), "the lists wait for each other"

        last = STEPS - 1
        vcopy, scopy = nc.vector.tensor_copy, nc.scalar.copy
        HALF = SEQ_BLOCKS // 2

        rounds = {2: [6], 3: [7], 4: [9, 10], 5: [11]}
        leaves = {5: [1], 6: [2, 3], 7: [4], 8: [5, 6], 9: [7], 10: [8], 11: [9]}
        FIRST_OUT = HID_BLOCKS
        SPLIT = (1, 5)
        OWN = 9

        tensor = [(idle_matmuls, [], []), (transpose_w_emb, [], ["w turned"]), turn_blocks(0, HALF), turn_blocks(HALF, HALF),
                  based(0, 1), based(1, 1), embed(0, 0), embed(0, 1), embed(1, 0), embed(1, 1), turn_blocks(SEQ_BLOCKS, SEQ_BLOCKS), embed(2), (bias_matmuls, [], ["biases summed"]),
                  based(3, 1), embed(3, 1), embed(3, 0)]
        scalar = [take_blocks(0, 1, scopy), take_blocks(1, 1, scopy, 0), take_blocks(HALF, HALF, scopy), rounded(0, 1), rounded(1, 1), take_blocks(SEQ_BLOCKS, SEQ_BLOCKS, scopy), rounded(3, 1)]
        vector = [(copy_w_emb, ["w turned"], ["w_emb_t"]), rounded(0, 0), rounded(1, 0), quantised(0, 1), quantised(1, 1),
                  (copy_biases, ["biases summed"], ["biases"]), rounded(2), rounded(3, 0), quantised(2, 1), quantised(3, 1), rounded(4), rounded(5)]
        gpsimd = []
        sync = []
        tensor.extend([gate(0, GATE_R, 0, HALF), gate(0, GATE_Z, 0, HALF), embed(4), gate(1, GATE_R, 0, HALF), gate(1, GATE_Z, 0, HALF),
                       gate(0, GATE_N, 0, HALF), embed(5)])
        tensor.extend([gate(0, GATE_R, HALF, HALF), gate(0, GATE_Z, HALF, HALF), gate(0, GATE_N, HALF, HALF), gate(1, GATE_R, HALF, HALF),
                       gate(1, GATE_Z, HALF, HALF)])
        for first in (0, HALF):
            for i in range(EARLY):
                scalar.extend([reset(i, first, HALF), update(i, first, HALF)])
        tensor.append(gate(1, GATE_N))
        vector.extend([summed(0), quantised(SEQ_BLOCKS, HALF), summed(1)])
        tensor.append(gate(EARLY, GATE_R))
        tensor.extend([embed(a) for i in range(EARLY, HID_BLOCKS) for a in rounds[i]])
        tensor.extend([gate(EARLY, GATE_N), gate(EARLY, GATE_Z)])
        scalar.append(tanh(0))
        gpsimd.append(state(0, nc.gpsimd))
        for i in range(EARLY, STEPS):
            if i >= HID_BLOCKS:
                tensor.extend([embed(a) for a in rounds.get(i, [])])
            if i + 1 == FIRST_OUT:
                tensor.extend([turn_back(0), embed(8)])
            tensor.extend([turn_back(k) for k in leaves.get(i, [])[:-1]])
            if i + 1 < last:
                tensor.extend(gates(i + 1))
                tensor.extend([turn_back(k) for k in leaves.get(i, [])[-1:]])
            elif i + 1 == last:
                tensor.extend([gate(last, GATE_R)] + [turn_back(k) for k in leaves[i]] + [gate(last, GATE_N), gate(last, GATE_Z)])
            else:
                tensor.extend([turn_back(k) for k in leaves[i]])
            if i == EARLY:
                tensor.append(turn_blocks(2 * SEQ_BLOCKS, SEQ_BLOCKS))
            scalar.extend([reset(i), tanh(i - 1), update(i)])
            if i - 1 < OWN:
                if i - 1 in SPLIT:
                    gpsimd.extend([state(i - 1, nc.gpsimd, first, HALF) for first in (0, HALF)])
                else:
                    gpsimd.append(state(i - 1, nc.gpsimd))
            early_round = i < HID_BLOCKS
            if i == FIRST_OUT:
                vector.extend([take_out(0, vcopy), rounded(8)])
                sync.append(stored(0, nc.sync))
            if not early_round:
                vector.append(summed(i))
                if i - 1 in rounds and rounds[i - 1][-1] == BLOCKS - 1:
                    vector.append(quantised(2 * SEQ_BLOCKS, SEQ_BLOCKS))
            vector.extend([rounded(a) for a in rounds.get(i, [])])
            if early_round:
                if i == HID_BLOCKS - 1:
                    vector.extend([take_blocks(2 * SEQ_BLOCKS, SEQ_BLOCKS, vcopy), quantised(rounds[i][0] - 1, 2)])
                vector.append(summed(i))
            if OWN <= i - 1 < last - 1:
                vector.append(state(i - 1, nc.vector))
            if i == last:
                for first in (0, HALF):
                    vector.append(state(i - 1, nc.vector, first, HALF))
                    tensor.append(turn_back(i - 1, first, HALF))
            for k in leaves.get(i, []):
                vector.append(take_out(k, vcopy))
                sync.append(stored(k, nc.sync))
                if k % HID_BLOCKS == HID_BLOCKS - 1:
                    sync.extend([stored_last(k // HID_BLOCKS, nc.sync, 0), stored_last(k // HID_BLOCKS, nc.sync, 1)])
        pieces = [WHOLE] + list(range(WHOLE))
        for a in pieces:
            scalar.append(tanh(last, a, 1))
            vector.append(state(last, nc.vector, a, 1))
        for a in pieces:
            tensor.append(turn_back(last, a, 1, True))
            vector.append(take_out(last, vcopy, a, 1))
        scalar.extend([take_out(last - 1, scopy, 0, HALF),
                       take_out(last - 1, scopy, HALF, HALF), stored(last - 1, nc.scalar), stored_last(BATCH - 1, nc.scalar, 0),
                       stored(last, nc.scalar, 0, 2), stored(last, nc.scalar, 2, 1)])
        sync.append(stored_last(BATCH - 1, nc.sync, 1))
        weave([tensor, scalar, vector, gpsimd, sync])
